import numpy as np
import ml_dtypes


def mxq(x, axis, fmt="e4m3"):
    dtype, down = {"e4m3": (ml_dtypes.float8_e4m3fn, 7), "e5m2": (ml_dtypes.float8_e5m2, 14)}[fmt]
    v = np.moveaxis(np.asarray(x, np.float32).astype(ml_dtypes.bfloat16).astype(np.float64), axis, -1)
    blocks = v.reshape(v.shape[:-1] + (-1, 32))
    amax = np.abs(blocks).max(-1, keepdims=True)
    byte = np.maximum(np.where(amax > 0, np.frexp(amax)[1] - 1 + 127, 0) - down, 1)
    scale = np.exp2(byte - 127.0)
    codes = (blocks / scale).astype(np.float32).astype(dtype).astype(np.float64)
    return np.moveaxis((codes * scale).reshape(v.shape), -1, axis)


WIDE = False


def mx_kscale(k):
    if not WIDE:
        return np.ones(k)
    levels = np.array([10, -10, 5, -5, 0])
    a = np.random.permutation(np.resize(levels, k // 512 * 4)).reshape(k // 512, 4)
    idx = np.arange(k)
    return np.exp2(a[idx // 512, idx % 128 // 32])


BF16 = ml_dtypes.bfloat16


def bf(x):
    return np.asarray(x, np.float32).astype(BF16)


def f64(x):
    return np.asarray(x).astype(np.float64)


E2M1 = np.array([0.0, 0.5, 1.0, 1.5, 2.0, 3.0, 4.0, 6.0, -0.0, -0.5, -1.0, -1.5, -2.0, -3.0, -4.0, -6.0])


def pack_weight(w, fmt):
    k, n = w.shape
    w = f64(bf(w)).reshape(k // 32, 32, n)
    amax = np.abs(w).max(1)
    if fmt == "e4m3":
        byte = np.frexp(amax)[1] - 1 + 127 - 7
    else:
        mant, ex = np.frexp(amax / 6.0)
        byte = np.where(mant > 0.5, ex, ex - 1) + 127
    byte = np.clip(np.where(amax > 0, byte, 1), 1, 254)
    scaled = (w * np.exp2(127.0 - byte)[:, None, :]).reshape(k, n).astype(np.float32)
    by_word = np.ascontiguousarray(scaled.reshape(k // 512, 128, 4, n).transpose(0, 1, 3, 2))
    if fmt == "e4m3":
        words = by_word.astype(ml_dtypes.float8_e4m3fn).view(np.uint8)
    else:
        c = by_word.astype(ml_dtypes.float4_e2m1fn).view(np.uint8) & 0xF
        words = c[..., 0::2] | (c[..., 1::2] << 4)
    return np.ascontiguousarray(words), np.ascontiguousarray(byte.astype(np.uint8).reshape(k // 512, 16, n))


def unpack_weight(words, scales, fmt):
    g, p, n, _ = words.shape
    if fmt == "e4m3":
        vals = np.ascontiguousarray(words).view(ml_dtypes.float8_e4m3fn).astype(np.float64)
    else:
        nib = np.empty((g, p, n, 4), np.uint8)
        nib[..., 0::2] = words & 0xF
        nib[..., 1::2] = words >> 4
        vals = E2M1[nib]
    vals = vals * np.repeat(np.exp2(scales.astype(np.float64) - 127.0), 8, axis=1)[..., None]
    return vals.transpose(0, 1, 3, 2).reshape(g * 512, n)


C, F, H, B, S = 2, 128, 1024, 2, 512
FMT = "e4m3"


def pack_stack(stack):
    st = np.swapaxes(stack, 1, 2)
    cat = st.reshape(-1, st.shape[-1])
    return pack_weight(cat, FMT)


def setup_inputs():
    s, t = mx_kscale(H), mx_kscale(H)
    g = 0.3 / np.sqrt(H)
    hidden = bf(np.random.standard_normal((B, S, H)) * s)
    emb_words, emb_scales = pack_stack(np.random.standard_normal((C, F, H)) * 0.3 * t)
    Wk_words, Wk_scales = pack_stack(np.random.standard_normal((C, H, H)) * g / t[:, None] / s)
    Wq_words, Wq_scales = pack_stack(np.random.standard_normal((C, H, H)) * g * t[:, None] / s)
    vsum = bf(np.random.standard_normal((C, B, S)))
    return {"hidden": hidden,
            "emb_words": emb_words, "emb_scales": emb_scales,
            "Wk_words": Wk_words, "Wk_scales": Wk_scales,
            "Wq_words": Wq_words, "Wq_scales": Wq_scales,
            "vsum": vsum}


def reference(hidden, emb_words, emb_scales, Wk_words, Wk_scales, Wq_words, Wq_scales, vsum):
    hq = mxq(f64(hidden), 2, "e4m3")[None]
    key = hq @ unpack_weight(Wk_words, Wk_scales, FMT).reshape(C, H, H)[:, None]
    query = hq @ unpack_weight(Wq_words, Wq_scales, FMT).reshape(C, H, H)[:, None]
    kt = mxq(key, 3, "e4m3").transpose(0, 1, 3, 2)
    att_tok = mxq(query, 3, "e4m3") @ kt
    att_lab = unpack_weight(emb_words, emb_scales, FMT).reshape(C, H, F).swapaxes(1, 2)[:, None] @ kt
    attention = np.concatenate([att_tok, att_lab], axis=2).transpose(1, 0, 2, 3)
    return attention * f64(vsum).transpose(1, 0, 2)[:, :, None, :]

@@ -1,0 +1,252 @@
+from contextlib import ExitStack
+
+import concourse.mybir as mybir
+from concourse.masks import make_identity
+
+F32 = mybir.dt.float32
+BF16 = mybir.dt.bfloat16
+I32 = mybir.dt.int32
+U32 = mybir.dt.uint32
+U8 = mybir.dt.uint8
+FP8X4 = mybir.dt.float8_e4m3fn_x4
+
+CHANNELS = 2
+BATCH = 2
+TOKENS = 512
+WIDTH = 1024
+LABELS = 128
+
+P = 128
+PACK = 4
+K_PASS = P * PACK
+PASSES = WIDTH // K_PASS
+TOKEN_TILES = TOKENS // P
+LABEL_TILE = TOKEN_TILES
+PLANE_ROWS = 4
+
+ROUND_TILES = 2
+ROUND_TOKENS = ROUND_TILES * P
+ROUNDS_PER_MATRIX = TOKEN_TILES // ROUND_TILES
+ROUNDS_PER_BATCH = CHANNELS * 2 * ROUNDS_PER_MATRIX
+
+HIDDEN_LEAD = 2
+FLIP_LAG = 1
+QUANTISE_LAG = 2
+SCORE_LAG = 3
+
+FLOPS = 2 * BATCH * CHANNELS * (2 * TOKENS * WIDTH * WIDTH + (TOKENS + LABELS) * WIDTH * TOKENS)
+
+
+def tile_relationtagger_pa_e_kernel(
+    tc, hidden, emb_words, emb_scales, Wk_words, Wk_scales, Wq_words, Wq_scales, vsum, out
+):
+    nc = tc.nc
+    with ExitStack() as ctx:
+        ctx.enter_context(tc.manual_schedule())
+        keep = ctx.enter_context(tc.tile_pool(name="keep", bufs=1))
+        work = ctx.enter_context(tc.tile_pool(name="work", bufs=2))
+        psum = ctx.enter_context(tc.psum_pool(name="psum", bufs=1))
+
+        hidden_sb = keep.tile([P, BATCH, TOKEN_TILES, WIDTH], BF16)
+        w_codes = {
+            "k": keep.tile([P, CHANNELS * PASSES, WIDTH], U32, name="wk_codes", align_bytes=64),
+            "q": keep.tile([P, CHANNELS * PASSES, WIDTH], U32, name="wq_codes", align_bytes=64),
+        }
+        emb_codes = keep.tile([P, CHANNELS * PASSES, LABELS], U32, align_bytes=64)
+        w_planes = {
+            "k": keep.tile([P, WIDTH], U8, name="wk_planes", align_bytes=64),
+            "q": keep.tile([P, WIDTH], U8, name="wq_planes", align_bytes=64),
+        }
+        emb_planes = keep.tile([P, LABELS], U8, align_bytes=64)
+        gate = keep.tile([P, CHANNELS, BATCH, TOKENS], BF16)
+        h_codes = keep.tile([P, PASSES, BATCH * TOKENS], U32, align_bytes=64)
+        h_planes = keep.tile([P, PASSES, BATCH * TOKENS], U8, align_bytes=64)
+        ident_f32 = keep.tile([P, P], F32)
+        ident_bf16 = keep.tile([P, P], BF16)
+
+        make_identity(nc, ident_f32[:])
+        make_identity(nc, ident_bf16[:])
+
+        for planes in (w_planes["k"], w_planes["q"], emb_planes):
+            nc.vector.memset(planes[:].bitcast(I32), 0)
+
+        def load_planes(planes, scales):
+            for quad in range(P // 32):
+                rows = slice(PLANE_ROWS * quad, PLANE_ROWS * (quad + 1))
+                nc.sync.dma_start(
+                    out=planes[32 * quad : 32 * quad + 16, :].bitcast(I32),
+                    in_=scales[:, rows, :].bitcast(I32),
+                )
+
+        def load_hidden(b):
+            for u in range(TOKEN_TILES):
+                nc.sync.dma_start(out=hidden_sb[:, b, u, :], in_=hidden[b, u * P : (u + 1) * P, :])
+
+        def load_weight(codes, words, c):
+            for g in range(PASSES):
+                n = c * PASSES + g
+                nc.sync.dma_start(
+                    out=codes[:, n, :].bitcast(I32),
+                    in_=words[n].rearrange("p n t -> p (n t)").bitcast(I32),
+                )
+
+        load_planes(w_planes["k"], Wk_scales)
+        load_hidden(0)
+        load_weight(w_codes["k"], Wk_words, 0)
+        load_planes(w_planes["q"], Wq_scales)
+        load_weight(w_codes["q"], Wq_words, 0)
+        load_planes(emb_planes, emb_scales)
+        nc.sync.dma_start(
+            out=emb_codes[:].bitcast(I32),
+            in_=emb_words.rearrange("g p n t -> p g (n t)").bitcast(I32),
+        )
+        load_weight(w_codes["k"], Wk_words, 1)
+        load_weight(w_codes["q"], Wq_words, 1)
+        load_hidden(1)
+        nc.sync.dma_start(
+            out=gate[:].rearrange("p c b s -> p (c b s)"),
+            in_=vsum.rearrange("c b s -> (c b s)").partition_broadcast(P),
+        )
+
+        def prepare_hidden(b):
+            grouped = work.tile([P, PASSES, TOKENS, PACK], BF16, name="h_grouped", bufs=1, align_bytes=64)
+            for u in range(TOKEN_TILES):
+                pairs = hidden_sb[:, b, u, :].bitcast(F32)
+                flipped = psum.tile([P, PASSES, 2, P], F32, name="h_flipped", tag="proj", bufs=4)
+                for g in range(PASSES):
+                    for h in range(2):
+                        first = (K_PASS // 2) * g + h
+                        nc.tensor.transpose(
+                            flipped[:, g, h, :], pairs[:, first : (K_PASS // 2) * (g + 1) : 2], ident_f32[:]
+                        )
+                copy = nc.scalar.copy if u % 2 == 0 else nc.vector.tensor_copy
+                copy(
+                    out=grouped[:, :, u * P : (u + 1) * P, :].bitcast(F32),
+                    in_=flipped[:].rearrange("p g h r -> p g r h"),
+                )
+            for g in range(PASSES):
+                cols = slice(b * TOKENS, (b + 1) * TOKENS)
+                nc.vector.quantize_mx(
+                    out=h_codes[:, g, cols].bitcast(FP8X4),
+                    scales=h_planes[:, g, cols],
+                    in_=grouped[:, g, :, :].rearrange("p s t -> p (s t)"),
+                )
+
+        rounded_of = {}
+        grouped_of = {}
+        codes_of = {}
+
+        def project(r):
+            b, c, which, part = r
+            rounded = work.tile([P, ROUND_TILES, PASSES, PACK, P], BF16, name="rounded", bufs=3)
+            rounded_of[r] = rounded
+            for a in range(ROUND_TILES):
+                first = b * TOKENS + (part * ROUND_TILES + a) * P
+                for s in range(PASSES):
+                    features = slice(s * K_PASS, (s + 1) * K_PASS)
+                    acc = psum.tile([P, K_PASS], F32, name="proj", bufs=4)
+                    for g in range(PASSES):
+                        n = c * PASSES + g
+                        nc.tensor.matmul_mx(
+                            out=acc[:],
+                            lhsT=h_codes[:, g, first : first + P].bitcast(FP8X4),
+                            lhsT_scale=h_planes[:, g, first : first + P],
+                            rhs=w_codes[which][:, n, features].bitcast(FP8X4),
+                            rhs_scale=w_planes[which][PLANE_ROWS * n : P, features],
+                            start=(g == 0),
+                            stop=(g == PASSES - 1),
+                        )
+                    nc.scalar.copy(
+                        out=rounded[:, a, s, :, :], in_=acc[:].rearrange("p (j t) -> p t j", t=PACK)
+                    )
+
+        def flip(r):
+            rounded = rounded_of[r]
+            grouped = work.tile([P, PASSES, ROUND_TOKENS, PACK], BF16, name="grouped", align_bytes=64)
+            grouped_of[r] = grouped
+            banks = []
+            for s in range(PASSES):
+                flipped = psum.tile([P, ROUND_TILES, PACK, P], BF16, name="flipped%d" % s)
+                banks.append(flipped)
+                for a in range(ROUND_TILES):
+                    for t in range(PACK):
+                        nc.tensor.transpose(flipped[:, a, t, :], rounded[:, a, s, t, :], ident_bf16[:])
+            for s in range(PASSES):
+                copy = nc.scalar.copy if s == 0 else nc.vector.tensor_copy
+                copy(
+                    out=grouped[:, s, :, :].rearrange("p (a r) t -> p a r t", a=ROUND_TILES),
+                    in_=banks[s][:].rearrange("p a t r -> p a r t"),
+                )
+
+        def quantise(r):
+            b, c, which, part = r
+            if part == 0:
+                codes_of[(b, c, which)] = (
+                    work.tile([P, PASSES, TOKENS], U32, name=which + "_codes", align_bytes=64),
+                    work.tile([P, PASSES, TOKENS], U8, name=which + "_planes", align_bytes=64),
+                )
+            codes, planes = codes_of[(b, c, which)]
+            grouped = grouped_of[r]
+            cols = slice(part * ROUND_TOKENS, (part + 1) * ROUND_TOKENS)
+            for s in range(PASSES):
+                nc.vector.quantize_mx(
+                    out=codes[:, s, cols].bitcast(FP8X4),
+                    scales=planes[:, s, cols],
+                    in_=grouped[:, s, :, :].rearrange("p r t -> p (r t)"),
+                )
+
+        def score(b, c, i):
+            k_codes, k_planes = codes_of[(b, c, "k")]
+            acc = psum.tile([P, TOKENS], F32, name="score", bufs=2)
+            for s in range(PASSES):
+                if i == LABEL_TILE:
+                    n = c * PASSES + s
+                    rows, rows_scale = emb_codes[:, n, :], emb_planes[PLANE_ROWS * n : P, :]
+                else:
+                    q_codes, q_planes = codes_of[(b, c, "q")]
+                    rows, rows_scale = q_codes[:, s, i * P : (i + 1) * P], q_planes[:, s, i * P : (i + 1) * P]
+                nc.tensor.matmul_mx(
+                    out=acc[:],
+                    lhsT=rows.bitcast(FP8X4),
+                    lhsT_scale=rows_scale,
+                    rhs=k_codes[:, s, :].bitcast(FP8X4),
+                    rhs_scale=k_planes[:, s, :],
+                    start=(s == 0),
+                    stop=(s == PASSES - 1),
+                )
+            gated = work.tile([P, TOKENS], F32, name="gated", bufs=4)
+            nc.vector.tensor_tensor(out=gated[:], in0=acc[:], in1=gate[:, c, b, :], op=mybir.AluOpType.mult)
+            nc.sync.dma_start(out=out[b, c, i * P : (i + 1) * P, :], in_=gated[:])
+
+        rounds = [
+            (b, c, which, part)
+            for b in range(BATCH)
+            for c in range(CHANNELS)
+            for which in ("k", "q")
+            for part in range(ROUNDS_PER_MATRIX)
+        ]
+
+        def round_at(n):
+            return rounds[n] if 0 <= n < len(rounds) else None
+
+        for n in range(-HIDDEN_LEAD, len(rounds) + SCORE_LAG):
+            r = round_at(n - QUANTISE_LAG)
+            if r is not None:
+                quantise(r)
+            r = round_at(n)
+            if r is not None:
+                project(r)
+            r = round_at(n - SCORE_LAG)
+            if r is not None:
+                b, c, which, part = r
+                if which == "q":
+                    for a in range(ROUND_TILES):
+                        score(b, c, part * ROUND_TILES + a)
+                elif part == ROUNDS_PER_MATRIX - 1:
+                    score(b, c, LABEL_TILE)
+            r = round_at(n - FLIP_LAG)
+            if r is not None:
+                flip(r)
+            r = round_at(n + HIDDEN_LEAD)
+            if r is not None and (n + HIDDEN_LEAD) % ROUNDS_PER_BATCH == 0:
+                prepare_hidden(r[0])

@@ -21,18 +21,11 @@ PACK = 4
 K_PASS = P * PACK
 PASSES = WIDTH // K_PASS
 TOKEN_TILES = TOKENS // P
-LABEL_TILE = TOKEN_TILES
 PLANE_ROWS = 4
+QUARTER = P // PACK
 
-ROUND_TILES = 2
-ROUND_TOKENS = ROUND_TILES * P
-ROUNDS_PER_MATRIX = TOKEN_TILES // ROUND_TILES
-ROUNDS_PER_BATCH = CHANNELS * 2 * ROUNDS_PER_MATRIX
-
-HIDDEN_LEAD = 2
-FLIP_LAG = 1
-QUANTISE_LAG = 2
-SCORE_LAG = 3
+PROJ_BANKS = 5
+SCORE_BANKS = 3
 
 FLOPS = 2 * BATCH * CHANNELS * (2 * TOKENS * WIDTH * WIDTH + (TOKENS + LABELS) * WIDTH * TOKENS)
 
@@ -62,10 +55,8 @@ def tile_relationtagger_pa_e_kernel(
         h_codes = keep.tile([P, PASSES, BATCH * TOKENS], U32, align_bytes=64)
         h_planes = keep.tile([P, PASSES, BATCH * TOKENS], U8, align_bytes=64)
         ident_f32 = keep.tile([P, P], F32)
-        ident_bf16 = keep.tile([P, P], BF16)
 
         make_identity(nc, ident_f32[:])
-        make_identity(nc, ident_bf16[:])
 
         for planes in (w_planes["k"], w_planes["q"], emb_planes):
             nc.vector.memset(planes[:].bitcast(I32), 0)
@@ -95,12 +86,12 @@ def tile_relationtagger_pa_e_kernel(
         load_weight(w_codes["k"], Wk_words, 0)
         load_planes(w_planes["q"], Wq_scales)
         load_weight(w_codes["q"], Wq_words, 0)
+        load_weight(w_codes["k"], Wk_words, 1)
         load_planes(emb_planes, emb_scales)
         nc.sync.dma_start(
             out=emb_codes[:].bitcast(I32),
             in_=emb_words.rearrange("g p n t -> p g (n t)").bitcast(I32),
         )
-        load_weight(w_codes["k"], Wk_words, 1)
         load_weight(w_codes["q"], Wq_words, 1)
         load_hidden(1)
         nc.sync.dma_start(
@@ -111,16 +102,15 @@ def tile_relationtagger_pa_e_kernel(
         def prepare_hidden(b):
             grouped = work.tile([P, PASSES, TOKENS, PACK], BF16, name="h_grouped", bufs=1, align_bytes=64)
             for u in range(TOKEN_TILES):
-                pairs = hidden_sb[:, b, u, :].bitcast(F32)
-                flipped = psum.tile([P, PASSES, 2, P], F32, name="h_flipped", tag="proj", bufs=4)
+                words = hidden_sb[:, b, u, :].bitcast(F32)
+                flipped = psum.tile([P, PASSES, 2, P], F32, name="h_flipped", tag="proj", bufs=PROJ_BANKS)
                 for g in range(PASSES):
                     for h in range(2):
                         first = (K_PASS // 2) * g + h
                         nc.tensor.transpose(
-                            flipped[:, g, h, :], pairs[:, first : (K_PASS // 2) * (g + 1) : 2], ident_f32[:]
+                            flipped[:, g, h, :], words[:, first : (K_PASS // 2) * (g + 1) : 2], ident_f32[:]
                         )
-                copy = nc.scalar.copy if u % 2 == 0 else nc.vector.tensor_copy
-                copy(
+                nc.scalar.copy(
                     out=grouped[:, :, u * P : (u + 1) * P, :].bitcast(F32),
                     in_=flipped[:].rearrange("p g h r -> p g r h"),
                 )
@@ -132,79 +122,94 @@ def tile_relationtagger_pa_e_kernel(
                     in_=grouped[:, g, :, :].rearrange("p s t -> p (s t)"),
                 )
 
-        rounded_of = {}
-        grouped_of = {}
-        codes_of = {}
+        def project_tile(acc, which, c, tile_index, tokens):
+            features = slice(tile_index * P, (tile_index + 1) * P)
+            for g in range(PASSES):
+                n = c * PASSES + g
+                nc.tensor.matmul_mx(
+                    out=acc,
+                    lhsT=w_codes[which][:, n, features].bitcast(FP8X4),
+                    lhsT_scale=w_planes[which][PLANE_ROWS * n : P, features],
+                    rhs=h_codes[:, g, tokens].bitcast(FP8X4),
+                    rhs_scale=h_planes[:, g, tokens],
+                    start=(g == 0),
+                    stop=(g == PASSES - 1),
+                )
 
-        def project(r):
-            b, c, which, part = r
-            rounded = work.tile([P, ROUND_TILES, PASSES, PACK, P], BF16, name="rounded", bufs=3)
-            rounded_of[r] = rounded
-            for a in range(ROUND_TILES):
-                first = b * TOKENS + (part * ROUND_TILES + a) * P
-                for s in range(PASSES):
-                    features = slice(s * K_PASS, (s + 1) * K_PASS)
-                    acc = psum.tile([P, K_PASS], F32, name="proj", bufs=4)
-                    for g in range(PASSES):
-                        n = c * PASSES + g
-                        nc.tensor.matmul_mx(
-                            out=acc[:],
-                            lhsT=h_codes[:, g, first : first + P].bitcast(FP8X4),
-                            lhsT_scale=h_planes[:, g, first : first + P],
-                            rhs=w_codes[which][:, n, features].bitcast(FP8X4),
-                            rhs_scale=w_planes[which][PLANE_ROWS * n : P, features],
-                            start=(g == 0),
-                            stop=(g == PASSES - 1),
-                        )
-                    nc.scalar.copy(
-                        out=rounded[:, a, s, :, :], in_=acc[:].rearrange("p (j t) -> p t j", t=PACK)
+        tiles_of = {}
+
+        def side_by_side(rows, s):
+            grouped = work.tile([P, TOKENS, PACK], BF16, name="k_grouped", bufs=3, align_bytes=64)
+            nc.vector.tensor_copy(
+                out=grouped[:].rearrange("p (n i) t -> p n t i", i=4),
+                in_=rows[:, s, :, :].rearrange("p t (n i) -> p n t i", i=4),
+            )
+            return grouped
+
+        def quantise_keys(grouped, codes, planes, s):
+            nc.vector.quantize_mx(
+                out=codes[:, s, :].bitcast(FP8X4),
+                scales=planes[:, s, :],
+                in_=grouped[:].rearrange("p r t -> p (r t)"),
+            )
+
+        def new_codes(b, c, name):
+            tiles_of[(b, c, name)] = (
+                work.tile([P, PASSES, TOKENS], U32, name=name + "_codes", align_bytes=64),
+                work.tile([P, PASSES, TOKENS], U8, name=name + "_planes", align_bytes=64),
+            )
+
+        def project_keys(b, c):
+            rows = work.tile([P, PASSES, PACK, TOKENS], BF16, name="k_rows")
+            moved = work.tile([P, PASSES, PACK, TOKENS], BF16, name="k_moved")
+            tiles_of[(b, c, "rows")] = rows
+            tiles_of[(b, c, "moved")] = moved
+            for s in range(PASSES):
+                for t in range(PACK):
+                    acc = psum.tile([P, TOKENS], F32, name="proj", bufs=PROJ_BANKS)
+                    project_tile(acc[:], "k", c, s * PACK + t, slice(b * TOKENS, (b + 1) * TOKENS))
+                    nc.scalar.copy(out=rows[:, s, t, :], in_=acc[:])
+                    nc.sync.dma_start(
+                        out=moved[QUARTER * t : QUARTER * (t + 1), s, :, :], in_=rows[:, s, t, :]
                     )
 
-        def flip(r):
-            rounded = rounded_of[r]
-            grouped = work.tile([P, PASSES, ROUND_TOKENS, PACK], BF16, name="grouped", align_bytes=64)
-            grouped_of[r] = grouped
-            banks = []
+        def quantise_tile_order_keys(b, c):
+            new_codes(b, c, "k_tile")
+            codes, planes = tiles_of[(b, c, "k_tile")]
+            grouped = [side_by_side(tiles_of[(b, c, "rows")], s) for s in range(PASSES)]
             for s in range(PASSES):
-                flipped = psum.tile([P, ROUND_TILES, PACK, P], BF16, name="flipped%d" % s)
-                banks.append(flipped)
-                for a in range(ROUND_TILES):
+                quantise_keys(grouped[s], codes, planes, s)
+
+        def quantise_packed_order_keys(b, c):
+            new_codes(b, c, "k_packed")
+            codes, planes = tiles_of[(b, c, "k_packed")]
+            grouped = [side_by_side(tiles_of[(b, c, "moved")], s) for s in range(PASSES)]
+            for s in range(PASSES):
+                quantise_keys(grouped[s], codes, planes, s)
+
+        def project_queries(b, c):
+            codes = work.tile([P, TOKEN_TILES, PASSES, P], U32, name="q_codes", align_bytes=64)
+            planes = work.tile([P, TOKEN_TILES, PASSES, P], U8, name="q_planes", align_bytes=64)
+            tiles_of[(b, c, "q")] = (codes, planes)
+            for u in range(TOKEN_TILES):
+                first = b * TOKENS + u * P
+                grouped = work.tile([P, PASSES, P, PACK], BF16, name="q_grouped", bufs=3, align_bytes=64)
+                for s in range(PASSES):
+                    acc = psum.tile([P, PACK, P], F32, name="q_proj", tag="proj", bufs=PROJ_BANKS)
                     for t in range(PACK):
-                        nc.tensor.transpose(flipped[:, a, t, :], rounded[:, a, s, t, :], ident_bf16[:])
-            for s in range(PASSES):
-                copy = nc.scalar.copy if s == 0 else nc.vector.tensor_copy
-                copy(
-                    out=grouped[:, s, :, :].rearrange("p (a r) t -> p a r t", a=ROUND_TILES),
-                    in_=banks[s][:].rearrange("p a t r -> p a r t"),
-                )
-
-        def quantise(r):
-            b, c, which, part = r
-            if part == 0:
-                codes_of[(b, c, which)] = (
-                    work.tile([P, PASSES, TOKENS], U32, name=which + "_codes", align_bytes=64),
-                    work.tile([P, PASSES, TOKENS], U8, name=which + "_planes", align_bytes=64),
-                )
-            codes, planes = codes_of[(b, c, which)]
-            grouped = grouped_of[r]
-            cols = slice(part * ROUND_TOKENS, (part + 1) * ROUND_TOKENS)
-            for s in range(PASSES):
+                        project_tile(acc[:, t, :], "q", c, s * PACK + t, slice(first, first + P))
+                    nc.scalar.copy(out=grouped[:, s, :, :], in_=acc[:].rearrange("p t r -> p r t"))
                 nc.vector.quantize_mx(
-                    out=codes[:, s, cols].bitcast(FP8X4),
-                    scales=planes[:, s, cols],
-                    in_=grouped[:, s, :, :].rearrange("p r t -> p (r t)"),
+                    out=codes[:, u, :, :].rearrange("p s r -> p (s r)").bitcast(FP8X4),
+                    scales=planes[:, u, :, :].rearrange("p s r -> p (s r)"),
+                    in_=grouped[:].rearrange("p s r t -> p (s r t)"),
                 )
 
-        def score(b, c, i):
-            k_codes, k_planes = codes_of[(b, c, "k")]
-            acc = psum.tile([P, TOKENS], F32, name="score", bufs=2)
+        def score_tile(b, c, first_row, rows_of_pass, keys):
+            k_codes, k_planes = keys
+            acc = psum.tile([P, TOKENS], F32, name="score", bufs=SCORE_BANKS)
             for s in range(PASSES):
-                if i == LABEL_TILE:
-                    n = c * PASSES + s
-                    rows, rows_scale = emb_codes[:, n, :], emb_planes[PLANE_ROWS * n : P, :]
-                else:
-                    q_codes, q_planes = codes_of[(b, c, "q")]
-                    rows, rows_scale = q_codes[:, s, i * P : (i + 1) * P], q_planes[:, s, i * P : (i + 1) * P]
+                rows, rows_scale = rows_of_pass(s)
                 nc.tensor.matmul_mx(
                     out=acc[:],
                     lhsT=rows.bitcast(FP8X4),
@@ -216,37 +221,31 @@ def tile_relationtagger_pa_e_kernel(
                 )
             gated = work.tile([P, TOKENS], F32, name="gated", bufs=4)
             nc.vector.tensor_tensor(out=gated[:], in0=acc[:], in1=gate[:, c, b, :], op=mybir.AluOpType.mult)
-            nc.sync.dma_start(out=out[b, c, i * P : (i + 1) * P, :], in_=gated[:])
+            nc.sync.dma_start(out=out[b, c, first_row : first_row + P, :], in_=gated[:])
 
-        rounds = [
-            (b, c, which, part)
-            for b in range(BATCH)
-            for c in range(CHANNELS)
-            for which in ("k", "q")
-            for part in range(ROUNDS_PER_MATRIX)
-        ]
+        def score(b, c):
+            q_codes, q_planes = tiles_of[(b, c, "q")]
+            for u in range(TOKEN_TILES):
+                score_tile(
+                    b, c, u * P, lambda s: (q_codes[:, u, s, :], q_planes[:, u, s, :]), tiles_of[(b, c, "k_tile")]
+                )
+            score_tile(
+                b,
+                c,
+                TOKENS,
+                lambda s: (emb_codes[:, c * PASSES + s, :], emb_planes[PLANE_ROWS * (c * PASSES + s) : P, :]),
+                tiles_of[(b, c, "k_packed")],
+            )
 
-        def round_at(n):
-            return rounds[n] if 0 <= n < len(rounds) else None
-
-        for n in range(-HIDDEN_LEAD, len(rounds) + SCORE_LAG):
-            r = round_at(n - QUANTISE_LAG)
-            if r is not None:
-                quantise(r)
-            r = round_at(n)
-            if r is not None:
-                project(r)
-            r = round_at(n - SCORE_LAG)
-            if r is not None:
-                b, c, which, part = r
-                if which == "q":
-                    for a in range(ROUND_TILES):
-                        score(b, c, part * ROUND_TILES + a)
-                elif part == ROUNDS_PER_MATRIX - 1:
-                    score(b, c, LABEL_TILE)
-            r = round_at(n - FLIP_LAG)
-            if r is not None:
-                flip(r)
-            r = round_at(n + HIDDEN_LEAD)
-            if r is not None and (n + HIDDEN_LEAD) % ROUNDS_PER_BATCH == 0:
-                prepare_hidden(r[0])
+        pairs = [(b, c) for b in range(BATCH) for c in range(CHANNELS)]
+        prepare_hidden(0)
+        for i, (b, c) in enumerate(pairs):
+            project_keys(b, c)
+            if i > 0:
+                score(*pairs[i - 1])
+            quantise_tile_order_keys(b, c)
+            if c == CHANNELS - 1 and b + 1 < BATCH:
+                prepare_hidden(b + 1)
+            quantise_packed_order_keys(b, c)
+            project_queries(b, c)
+        score(*pairs[-1])

@@ -139,7 +139,7 @@ def tile_relationtagger_pa_e_kernel(
         tiles_of = {}
 
         def side_by_side(rows, s):
-            grouped = work.tile([P, TOKENS, PACK], BF16, name="k_grouped", bufs=3, align_bytes=64)
+            grouped = work.tile([P, TOKENS, PACK], BF16, name="k_grouped", bufs=4, align_bytes=64)
             nc.vector.tensor_copy(
                 out=grouped[:].rearrange("p (n i) t -> p n t i", i=4),
                 in_=rows[:, s, :, :].rearrange("p t (n i) -> p n t i", i=4),
@@ -173,13 +173,6 @@ def tile_relationtagger_pa_e_kernel(
                         out=moved[QUARTER * t : QUARTER * (t + 1), s, :, :], in_=rows[:, s, t, :]
                     )
 
-        def quantise_tile_order_keys(b, c):
-            new_codes(b, c, "k_tile")
-            codes, planes = tiles_of[(b, c, "k_tile")]
-            grouped = [side_by_side(tiles_of[(b, c, "rows")], s) for s in range(PASSES)]
-            for s in range(PASSES):
-                quantise_keys(grouped[s], codes, planes, s)
-
         def quantise_packed_order_keys(b, c):
             new_codes(b, c, "k_packed")
             codes, planes = tiles_of[(b, c, "k_packed")]
@@ -188,12 +181,15 @@ def tile_relationtagger_pa_e_kernel(
                 quantise_keys(grouped[s], codes, planes, s)
 
         def project_queries(b, c):
+            new_codes(b, c, "k_tile")
+            k_codes, k_planes = tiles_of[(b, c, "k_tile")]
+            k_grouped = [side_by_side(tiles_of[(b, c, "rows")], s) for s in range(PASSES)]
             codes = work.tile([P, TOKEN_TILES, PASSES, P], U32, name="q_codes", align_bytes=64)
             planes = work.tile([P, TOKEN_TILES, PASSES, P], U8, name="q_planes", align_bytes=64)
             tiles_of[(b, c, "q")] = (codes, planes)
             for u in range(TOKEN_TILES):
                 first = b * TOKENS + u * P
-                grouped = work.tile([P, PASSES, P, PACK], BF16, name="q_grouped", bufs=3, align_bytes=64)
+                grouped = work.tile([P, PASSES, P, PACK], BF16, name="q_grouped", bufs=4, align_bytes=64)
                 for s in range(PASSES):
                     acc = psum.tile([P, PACK, P], F32, name="q_proj", tag="proj", bufs=PROJ_BANKS)
                     for t in range(PACK):
@@ -204,6 +200,8 @@ def tile_relationtagger_pa_e_kernel(
                     scales=planes[:, u, :, :].rearrange("p s r -> p (s r)"),
                     in_=grouped[:].rearrange("p s r t -> p (s r t)"),
                 )
+                if u < PASSES:
+                    quantise_keys(k_grouped[u], k_codes, k_planes, u)
 
         def score_tile(b, c, first_row, rows_of_pass, keys):
             k_codes, k_planes = keys
@@ -242,10 +240,10 @@ def tile_relationtagger_pa_e_kernel(
         for i, (b, c) in enumerate(pairs):
             project_keys(b, c)
             if i > 0:
+                quantise_packed_order_keys(*pairs[i - 1])
                 score(*pairs[i - 1])
-            quantise_tile_order_keys(b, c)
             if c == CHANNELS - 1 and b + 1 < BATCH:
                 prepare_hidden(b + 1)
-            quantise_packed_order_keys(b, c)
             project_queries(b, c)
+        quantise_packed_order_keys(*pairs[-1])
         score(*pairs[-1])

@@ -81,26 +81,32 @@ def tile_relationtagger_pa_e_kernel(
                     in_=words[n].rearrange("p n t -> p (n t)").bitcast(I32),
                 )
 
-        load_planes(w_planes["k"], Wk_scales)
-        load_hidden(0)
-        load_weight(w_codes["k"], Wk_words, 0)
-        load_planes(w_planes["q"], Wq_scales)
-        load_weight(w_codes["q"], Wq_words, 0)
-        load_weight(w_codes["k"], Wk_words, 1)
-        load_planes(emb_planes, emb_scales)
-        nc.sync.dma_start(
-            out=emb_codes[:].bitcast(I32),
-            in_=emb_words.rearrange("g p n t -> p g (n t)").bitcast(I32),
-        )
-        load_weight(w_codes["q"], Wq_words, 1)
-        load_hidden(1)
-        nc.sync.dma_start(
-            out=gate[:].rearrange("p c b s -> p (c b s)"),
-            in_=vsum.rearrange("c b s -> (c b s)").partition_broadcast(P),
-        )
+        def load_what_the_first_steps_need():
+            load_planes(w_planes["k"], Wk_scales)
+            load_hidden(0)
+            load_weight(w_codes["k"], Wk_words, 0)
+            load_weight(w_codes["k"], Wk_words, 1)
+            load_planes(w_planes["q"], Wq_scales)
+            load_weight(w_codes["q"], Wq_words, 0)
+            load_hidden(1)
 
-        def prepare_hidden(b):
+        def load_the_rest():
+            load_planes(emb_planes, emb_scales)
+            nc.sync.dma_start(
+                out=emb_codes[:].bitcast(I32),
+                in_=emb_words.rearrange("g p n t -> p g (n t)").bitcast(I32),
+            )
+            nc.sync.dma_start(
+                out=gate[:].rearrange("p c b s -> p (c b s)"),
+                in_=vsum.rearrange("c b s -> (c b s)").partition_broadcast(P),
+            )
+            load_weight(w_codes["q"], Wq_words, 1)
+
+        tiles_of = {}
+
+        def flip_hidden(b):
             grouped = work.tile([P, PASSES, TOKENS, PACK], BF16, name="h_grouped", bufs=1, align_bytes=64)
+            tiles_of[(b, "hidden")] = grouped
             for u in range(TOKEN_TILES):
                 words = hidden_sb[:, b, u, :].bitcast(F32)
                 flipped = psum.tile([P, PASSES, 2, P], F32, name="h_flipped", tag="proj", bufs=PROJ_BANKS)
@@ -114,13 +120,17 @@ def tile_relationtagger_pa_e_kernel(
                     out=grouped[:, :, u * P : (u + 1) * P, :].bitcast(F32),
                     in_=flipped[:].rearrange("p g h r -> p g r h"),
                 )
-            for g in range(PASSES):
-                cols = slice(b * TOKENS, (b + 1) * TOKENS)
-                nc.vector.quantize_mx(
-                    out=h_codes[:, g, cols].bitcast(FP8X4),
-                    scales=h_planes[:, g, cols],
-                    in_=grouped[:, g, :, :].rearrange("p s t -> p (s t)"),
-                )
+
+        def quantise_hidden(b):
+            grouped = tiles_of[(b, "hidden")]
+            for u in range(TOKEN_TILES):
+                for g in range(PASSES):
+                    cols = slice(b * TOKENS + u * P, b * TOKENS + (u + 1) * P)
+                    nc.vector.quantize_mx(
+                        out=h_codes[:, g, cols].bitcast(FP8X4),
+                        scales=h_planes[:, g, cols],
+                        in_=grouped[:, g, u * P : (u + 1) * P, :].rearrange("p s t -> p (s t)"),
+                    )
 
         def project_tile(acc, which, c, tile_index, tokens):
             features = slice(tile_index * P, (tile_index + 1) * P)
@@ -135,8 +145,6 @@ def tile_relationtagger_pa_e_kernel(
                     start=(g == 0),
                     stop=(g == PASSES - 1),
                 )
-
-        tiles_of = {}
 
         def side_by_side(rows, s):
             grouped = work.tile([P, TOKENS, PACK], BF16, name="k_grouped", bufs=4, align_bytes=64)
@@ -173,17 +181,19 @@ def tile_relationtagger_pa_e_kernel(
                         out=moved[QUARTER * t : QUARTER * (t + 1), s, :, :], in_=rows[:, s, t, :]
                     )
 
-        def quantise_packed_order_keys(b, c):
-            new_codes(b, c, "k_packed")
-            codes, planes = tiles_of[(b, c, "k_packed")]
-            grouped = [side_by_side(tiles_of[(b, c, "moved")], s) for s in range(PASSES)]
+        def quantise_key_copy(b, c, source, name):
+            new_codes(b, c, name)
+            codes, planes = tiles_of[(b, c, name)]
+            grouped = [side_by_side(tiles_of[(b, c, source)], s) for s in range(PASSES)]
             for s in range(PASSES):
                 quantise_keys(grouped[s], codes, planes, s)
 
-        def project_queries(b, c):
-            new_codes(b, c, "k_tile")
-            k_codes, k_planes = tiles_of[(b, c, "k_tile")]
-            k_grouped = [side_by_side(tiles_of[(b, c, "rows")], s) for s in range(PASSES)]
+        def project_queries(b, c, ahead):
+            if ahead is not None:
+                new_codes(ahead[0], ahead[1], "k_tile")
+                k_codes, k_planes = tiles_of[(ahead[0], ahead[1], "k_tile")]
+                k_rows = tiles_of[(ahead[0], ahead[1], "rows")]
+                k_grouped = []
             codes = work.tile([P, TOKEN_TILES, PASSES, P], U32, name="q_codes", align_bytes=64)
             planes = work.tile([P, TOKEN_TILES, PASSES, P], U8, name="q_planes", align_bytes=64)
             tiles_of[(b, c, "q")] = (codes, planes)
@@ -195,13 +205,15 @@ def tile_relationtagger_pa_e_kernel(
                     for t in range(PACK):
                         project_tile(acc[:, t, :], "q", c, s * PACK + t, slice(first, first + P))
                     nc.scalar.copy(out=grouped[:, s, :, :], in_=acc[:].rearrange("p t r -> p r t"))
+                if ahead is not None and u < PASSES:
+                    k_grouped.append(side_by_side(k_rows, u))
+                elif ahead is not None:
+                    quantise_keys(k_grouped[u - PASSES], k_codes, k_planes, u - PASSES)
                 nc.vector.quantize_mx(
                     out=codes[:, u, :, :].rearrange("p s r -> p (s r)").bitcast(FP8X4),
                     scales=planes[:, u, :, :].rearrange("p s r -> p (s r)"),
                     in_=grouped[:].rearrange("p s r t -> p (s r t)"),
                 )
-                if u < PASSES:
-                    quantise_keys(k_grouped[u], k_codes, k_planes, u)
 
         def score_tile(b, c, first_row, rows_of_pass, keys):
             k_codes, k_planes = keys
@@ -217,16 +229,11 @@ def tile_relationtagger_pa_e_kernel(
                     start=(s == 0),
                     stop=(s == PASSES - 1),
                 )
-            gated = work.tile([P, TOKENS], F32, name="gated", bufs=4)
+            gated = work.tile([P, TOKENS], F32, name="gated", bufs=6)
             nc.vector.tensor_tensor(out=gated[:], in0=acc[:], in1=gate[:, c, b, :], op=mybir.AluOpType.mult)
             nc.sync.dma_start(out=out[b, c, first_row : first_row + P, :], in_=gated[:])
 
         def score(b, c):
-            q_codes, q_planes = tiles_of[(b, c, "q")]
-            for u in range(TOKEN_TILES):
-                score_tile(
-                    b, c, u * P, lambda s: (q_codes[:, u, s, :], q_planes[:, u, s, :]), tiles_of[(b, c, "k_tile")]
-                )
             score_tile(
                 b,
                 c,
@@ -234,16 +241,32 @@ def tile_relationtagger_pa_e_kernel(
                 lambda s: (emb_codes[:, c * PASSES + s, :], emb_planes[PLANE_ROWS * (c * PASSES + s) : P, :]),
                 tiles_of[(b, c, "k_packed")],
             )
+            q_codes, q_planes = tiles_of[(b, c, "q")]
+            for u in range(TOKEN_TILES):
+                score_tile(
+                    b, c, u * P, lambda s: (q_codes[:, u, s, :], q_planes[:, u, s, :]), tiles_of[(b, c, "k_tile")]
+                )
 
         pairs = [(b, c) for b in range(BATCH) for c in range(CHANNELS)]
-        prepare_hidden(0)
+
+        def pair_at(i):
+            return pairs[i] if i < len(pairs) else None
+
+        load_what_the_first_steps_need()
+        flip_hidden(0)
+        quantise_hidden(0)
+        project_keys(*pairs[0])
+        load_the_rest()
+        quantise_key_copy(*pairs[0], "rows", "k_tile")
         for i, (b, c) in enumerate(pairs):
-            project_keys(b, c)
-            if i > 0:
-                quantise_packed_order_keys(*pairs[i - 1])
-                score(*pairs[i - 1])
-            if c == CHANNELS - 1 and b + 1 < BATCH:
-                prepare_hidden(b + 1)
-            project_queries(b, c)
-        quantise_packed_order_keys(*pairs[-1])
-        score(*pairs[-1])
+            ahead = pair_at(i + 1)
+            new_batch = pair_at(i + 2) is not None and pair_at(i + 2)[1] == 0
+            if ahead is not None:
+                project_keys(*ahead)
+            quantise_key_copy(b, c, "moved", "k_packed")
+            if new_batch:
+                flip_hidden(pair_at(i + 2)[0])
+            project_queries(b, c, ahead)
+            if new_batch:
+                quantise_hidden(pair_at(i + 2)[0])
+            score(b, c)

@@ -74,16 +74,18 @@ def tile_relationtagger_pa_e_kernel(
                 nc.sync.dma_start(out=hidden_sb[:, b, u, :], in_=hidden[b, u * P : (u + 1) * P, :])
 
         def load_weight(codes, words, c):
-            for g in range(PASSES):
-                n = c * PASSES + g
-                nc.sync.dma_start(
-                    out=codes[:, n, :].bitcast(I32),
-                    in_=words[n].rearrange("p n t -> p (n t)").bitcast(I32),
-                )
+            for s in range(PASSES):
+                features = slice(s * K_PASS, (s + 1) * K_PASS)
+                for g in range(PASSES):
+                    n = c * PASSES + g
+                    nc.sync.dma_start(
+                        out=codes[:, n, features].bitcast(I32),
+                        in_=words[n, :, features, :].rearrange("p n t -> p (n t)").bitcast(I32),
+                    )
 
         def load_what_the_first_steps_need():
-            load_planes(w_planes["k"], Wk_scales)
             load_hidden(0)
+            load_planes(w_planes["k"], Wk_scales)
             load_weight(w_codes["k"], Wk_words, 0)
             load_weight(w_codes["k"], Wk_words, 1)
             load_planes(w_planes["q"], Wq_scales)

@@ -51,12 +51,16 @@ def tile_relationtagger_pa_e_kernel(
             "q": keep.tile([P, WIDTH], U8, name="wq_planes", align_bytes=64),
         }
         emb_planes = keep.tile([P, LABELS], U8, align_bytes=64)
-        gate = keep.tile([P, CHANNELS, BATCH, TOKENS], BF16)
+        gate_row = keep.tile([P, CHANNELS, BATCH, TOKENS], BF16)
+        gate = keep.tile([P, CHANNELS, BATCH, TOKENS], F32)
+        ones = keep.tile([P, P], BF16)
         h_codes = keep.tile([P, PASSES, BATCH * TOKENS], U32, align_bytes=64)
         h_planes = keep.tile([P, PASSES, BATCH * TOKENS], U8, align_bytes=64)
         ident_f32 = keep.tile([P, P], F32)
 
         make_identity(nc, ident_f32[:])
+        nc.gpsimd.memset(ones[:], 1.0)
+        nc.vector.memset(gate_row[:].bitcast(I32), 0)
 
         for planes in (w_planes["k"], w_planes["q"], emb_planes):
             nc.vector.memset(planes[:].bitcast(I32), 0)
@@ -74,17 +78,16 @@ def tile_relationtagger_pa_e_kernel(
                 nc.sync.dma_start(out=hidden_sb[:, b, u, :], in_=hidden[b, u * P : (u + 1) * P, :])
 
         def load_weight(codes, words, c):
-            for s in range(PASSES):
-                features = slice(s * K_PASS, (s + 1) * K_PASS)
-                for g in range(PASSES):
-                    n = c * PASSES + g
-                    nc.sync.dma_start(
-                        out=codes[:, n, features].bitcast(I32),
-                        in_=words[n, :, features, :].rearrange("p n t -> p (n t)").bitcast(I32),
-                    )
+            for g in range(PASSES):
+                n = c * PASSES + g
+                nc.sync.dma_start(
+                    out=codes[:, n, :].bitcast(I32),
+                    in_=words[n].rearrange("p n t -> p (n t)").bitcast(I32),
+                )
 
         def load_what_the_first_steps_need():
             load_hidden(0)
+            nc.sync.dma_start(out=gate_row[0:1], in_=vsum.unsqueeze(0))
             load_planes(w_planes["k"], Wk_scales)
             load_weight(w_codes["k"], Wk_words, 0)
             load_weight(w_codes["k"], Wk_words, 1)
@@ -97,10 +100,6 @@ def tile_relationtagger_pa_e_kernel(
             nc.sync.dma_start(
                 out=emb_codes[:].bitcast(I32),
                 in_=emb_words.rearrange("g p n t -> p g (n t)").bitcast(I32),
-            )
-            nc.sync.dma_start(
-                out=gate[:].rearrange("p c b s -> p (c b s)"),
-                in_=vsum.rearrange("c b s -> (c b s)").partition_broadcast(P),
             )
             load_weight(w_codes["q"], Wq_words, 1)
 
@@ -133,6 +132,13 @@ def tile_relationtagger_pa_e_kernel(
                         scales=h_planes[:, g, cols],
                         in_=grouped[:, g, u * P : (u + 1) * P, :].rearrange("p s t -> p (s t)"),
                     )
+
+        def spread_gate():
+            for c in range(CHANNELS):
+                for b in range(BATCH):
+                    acc = psum.tile([P, TOKENS], F32, name="gate_acc", tag="proj", bufs=PROJ_BANKS)
+                    nc.tensor.matmul(out=acc[:], lhsT=ones[:], rhs=gate_row[:, c, b, :], start=True, stop=True)
+                    nc.vector.tensor_copy(out=gate[:, c, b, :], in_=acc[:])
 
         def project_tile(acc, which, c, tile_index, tokens):
             features = slice(tile_index * P, (tile_index + 1) * P)
@@ -257,6 +263,7 @@ def tile_relationtagger_pa_e_kernel(
         load_what_the_first_steps_need()
         flip_hidden(0)
         quantise_hidden(0)
+        spread_gate()
         project_keys(*pairs[0])
         load_the_rest()
         quantise_key_copy(*pairs[0], "rows", "k_tile")

@@ -22,7 +22,7 @@ K_PASS = P * PACK
 PASSES = WIDTH // K_PASS
 TOKEN_TILES = TOKENS // P
 PLANE_ROWS = 4
-QUARTER = P // PACK
+UNITS = TOKEN_TILES * PASSES
 
 PROJ_BANKS = 5
 SCORE_BANKS = 3
@@ -41,28 +41,31 @@ def tile_relationtagger_pa_e_kernel(
         psum = ctx.enter_context(tc.psum_pool(name="psum", bufs=1))
 
         hidden_sb = keep.tile([P, BATCH, TOKEN_TILES, WIDTH], BF16)
+        raw_codes = {
+            "k": keep.tile([P, CHANNELS * PASSES, WIDTH], U32, name="wk_raw", align_bytes=64),
+            "q": keep.tile([P, CHANNELS * PASSES, WIDTH], U32, name="wq_raw", align_bytes=64),
+        }
         w_codes = {
             "k": keep.tile([P, CHANNELS * PASSES, WIDTH], U32, name="wk_codes", align_bytes=64),
             "q": keep.tile([P, CHANNELS * PASSES, WIDTH], U32, name="wq_codes", align_bytes=64),
         }
         emb_codes = keep.tile([P, CHANNELS * PASSES, LABELS], U32, align_bytes=64)
+        raw_planes = {
+            "k": keep.tile([P, WIDTH], U8, name="wk_raw_planes", align_bytes=64),
+            "q": keep.tile([P, WIDTH], U8, name="wq_raw_planes", align_bytes=64),
+        }
         w_planes = {
             "k": keep.tile([P, WIDTH], U8, name="wk_planes", align_bytes=64),
             "q": keep.tile([P, WIDTH], U8, name="wq_planes", align_bytes=64),
         }
         emb_planes = keep.tile([P, LABELS], U8, align_bytes=64)
-        gate_row = keep.tile([P, CHANNELS, BATCH, TOKENS], BF16)
-        gate = keep.tile([P, CHANNELS, BATCH, TOKENS], F32)
-        ones = keep.tile([P, P], BF16)
+        gate = keep.tile([P, CHANNELS, BATCH, TOKENS], BF16)
         h_codes = keep.tile([P, PASSES, BATCH * TOKENS], U32, align_bytes=64)
         h_planes = keep.tile([P, PASSES, BATCH * TOKENS], U8, align_bytes=64)
         ident_f32 = keep.tile([P, P], F32)
 
         make_identity(nc, ident_f32[:])
-        nc.gpsimd.memset(ones[:], 1.0)
-        nc.vector.memset(gate_row[:].bitcast(I32), 0)
-
-        for planes in (w_planes["k"], w_planes["q"], emb_planes):
+        for planes in (raw_planes["k"], raw_planes["q"], emb_planes):
             nc.vector.memset(planes[:].bitcast(I32), 0)
 
         def load_planes(planes, scales):
@@ -73,161 +76,152 @@ def tile_relationtagger_pa_e_kernel(
                     in_=scales[:, rows, :].bitcast(I32),
                 )
 
-        def load_hidden(b):
-            for u in range(TOKEN_TILES):
-                nc.sync.dma_start(out=hidden_sb[:, b, u, :], in_=hidden[b, u * P : (u + 1) * P, :])
+        def load_hidden(b, u):
+            nc.sync.dma_start(out=hidden_sb[:, b, u, :], in_=hidden[b, u * P : (u + 1) * P, :])
 
-        def load_weight(codes, words, c):
+        def load_weight(which, words, c, s):
             for g in range(PASSES):
                 n = c * PASSES + g
+                cols = slice(s * K_PASS, (s + 1) * K_PASS)
                 nc.sync.dma_start(
-                    out=codes[:, n, :].bitcast(I32),
-                    in_=words[n].rearrange("p n t -> p (n t)").bitcast(I32),
+                    out=raw_codes[which][:, n, cols].bitcast(I32),
+                    in_=words[n].rearrange("p n t -> p (n t)").bitcast(I32)[:, cols],
                 )
 
-        def load_what_the_first_steps_need():
-            load_hidden(0)
-            nc.sync.dma_start(out=gate_row[0:1], in_=vsum.unsqueeze(0))
-            load_planes(w_planes["k"], Wk_scales)
-            load_weight(w_codes["k"], Wk_words, 0)
-            load_weight(w_codes["k"], Wk_words, 1)
-            load_planes(w_planes["q"], Wq_scales)
-            load_weight(w_codes["q"], Wq_words, 0)
-            load_hidden(1)
-
-        def load_the_rest():
+        def load_all():
+            load_hidden(0, 0)
+            load_planes(raw_planes["k"], Wk_scales)
+            load_weight("k", Wk_words, 0, 0)
+            load_hidden(0, 1)
+            load_weight("k", Wk_words, 0, 1)
+            load_hidden(0, 2)
+            load_hidden(0, 3)
+            load_planes(raw_planes["q"], Wq_scales)
+            load_weight("q", Wq_words, 0, 0)
+            load_weight("q", Wq_words, 0, 1)
+            load_weight("k", Wk_words, 1, 0)
+            load_weight("k", Wk_words, 1, 1)
+            nc.sync.dma_start(
+                out=gate[:].rearrange("p c b t -> p (c b t)"),
+                in_=vsum.rearrange("c b t -> (c b t)").partition_broadcast(P),
+            )
             load_planes(emb_planes, emb_scales)
             nc.sync.dma_start(
                 out=emb_codes[:].bitcast(I32),
                 in_=emb_words.rearrange("g p n t -> p g (n t)").bitcast(I32),
             )
-            load_weight(w_codes["q"], Wq_words, 1)
+            for u in range(TOKEN_TILES):
+                load_hidden(1, u)
+            load_weight("q", Wq_words, 1, 0)
+            load_weight("q", Wq_words, 1, 1)
+
+        def sort_planes(which, s):
+            cols = slice(s * K_PASS, (s + 1) * K_PASS)
+            nc.vector.tensor_copy(
+                out=w_planes[which][:, cols].rearrange("p (t n i) -> p n t i", t=PACK, i=16),
+                in_=raw_planes[which][:, cols].rearrange("p (n i t) -> p n t i", t=PACK, i=16),
+            )
+
+        def sort_words(which, c, s, g):
+            n = c * PASSES + g
+            cols = slice(s * K_PASS, (s + 1) * K_PASS)
+            nc.vector.tensor_copy(
+                out=w_codes[which][:, n, cols].bitcast(I32).rearrange("p (t n i) -> p n t i", t=PACK, i=4),
+                in_=raw_codes[which][:, n, cols].bitcast(I32).rearrange("p (n i t) -> p n t i", t=PACK, i=4),
+            )
+
+        h_grouped = {}
+
+        def flip_hidden(b, u):
+            grouped = work.tile([P, PASSES, P, PACK], BF16, name="h_grouped", bufs=4, align_bytes=64)
+            h_grouped[(b, u)] = grouped
+            words = hidden_sb[:, b, u, :].bitcast(F32)
+            flipped = psum.tile([P, PASSES, 2, P], F32, name="h_flipped", tag="proj", bufs=PROJ_BANKS)
+            for g in range(PASSES):
+                for h in range(2):
+                    first = (K_PASS // 2) * g + h
+                    nc.tensor.transpose(
+                        flipped[:, g, h, :], words[:, first : (K_PASS // 2) * (g + 1) : 2], ident_f32[:]
+                    )
+            nc.scalar.copy(
+                out=grouped[:].bitcast(F32),
+                in_=flipped[:].rearrange("p g h r -> p g r h"),
+            )
+
+        def quantise_hidden(b, u):
+            for g in range(PASSES):
+                cols = slice(b * TOKENS + u * P, b * TOKENS + (u + 1) * P)
+                nc.vector.quantize_mx(
+                    out=h_codes[:, g, cols].bitcast(FP8X4),
+                    scales=h_planes[:, g, cols],
+                    in_=h_grouped[(b, u)][:, g, :, :].rearrange("p s t -> p (s t)"),
+                )
+
+        def project(which, b, c, u, s, grouped):
+            tokens = slice(b * TOKENS + u * P, b * TOKENS + (u + 1) * P)
+            acc = psum.tile([P, PACK, P], F32, name="proj", bufs=PROJ_BANKS)
+            for t in range(PACK):
+                features = slice(s * K_PASS + t * P, s * K_PASS + (t + 1) * P)
+                for g in range(PASSES):
+                    n = c * PASSES + g
+                    nc.tensor.matmul_mx(
+                        out=acc[:, t, :],
+                        lhsT=w_codes[which][:, n, features].bitcast(FP8X4),
+                        lhsT_scale=w_planes[which][PLANE_ROWS * n : P, features],
+                        rhs=h_codes[:, g, tokens].bitcast(FP8X4),
+                        rhs_scale=h_planes[:, g, tokens],
+                        start=(g == 0),
+                        stop=(g == PASSES - 1),
+                    )
+            nc.scalar.copy(out=grouped, in_=acc[:].rearrange("p t r -> p r t"))
 
         tiles_of = {}
 
-        def flip_hidden(b):
-            grouped = work.tile([P, PASSES, TOKENS, PACK], BF16, name="h_grouped", bufs=1, align_bytes=64)
-            tiles_of[(b, "hidden")] = grouped
-            for u in range(TOKEN_TILES):
-                words = hidden_sb[:, b, u, :].bitcast(F32)
-                flipped = psum.tile([P, PASSES, 2, P], F32, name="h_flipped", tag="proj", bufs=PROJ_BANKS)
-                for g in range(PASSES):
-                    for h in range(2):
-                        first = (K_PASS // 2) * g + h
-                        nc.tensor.transpose(
-                            flipped[:, g, h, :], words[:, first : (K_PASS // 2) * (g + 1) : 2], ident_f32[:]
-                        )
-                nc.scalar.copy(
-                    out=grouped[:, :, u * P : (u + 1) * P, :].bitcast(F32),
-                    in_=flipped[:].rearrange("p g h r -> p g r h"),
+        def key_unit(i, u, s):
+            b, c = pairs[i]
+            if (u, s) == (0, 0):
+                tiles_of[(i, "k")] = (
+                    work.tile([P, PASSES, TOKENS, PACK], BF16, name="k_grouped", align_bytes=64),
+                    work.tile([P, PASSES, TOKENS], U32, name="k_codes", align_bytes=64),
+                    work.tile([P, PASSES, TOKENS], U8, name="k_planes", align_bytes=64),
                 )
-
-        def quantise_hidden(b):
-            grouped = tiles_of[(b, "hidden")]
-            for u in range(TOKEN_TILES):
-                for g in range(PASSES):
-                    cols = slice(b * TOKENS + u * P, b * TOKENS + (u + 1) * P)
-                    nc.vector.quantize_mx(
-                        out=h_codes[:, g, cols].bitcast(FP8X4),
-                        scales=h_planes[:, g, cols],
-                        in_=grouped[:, g, u * P : (u + 1) * P, :].rearrange("p s t -> p (s t)"),
-                    )
-
-        def spread_gate():
-            for c in range(CHANNELS):
-                for b in range(BATCH):
-                    acc = psum.tile([P, TOKENS], F32, name="gate_acc", tag="proj", bufs=PROJ_BANKS)
-                    nc.tensor.matmul(out=acc[:], lhsT=ones[:], rhs=gate_row[:, c, b, :], start=True, stop=True)
-                    nc.vector.tensor_copy(out=gate[:, c, b, :], in_=acc[:])
-
-        def project_tile(acc, which, c, tile_index, tokens):
-            features = slice(tile_index * P, (tile_index + 1) * P)
-            for g in range(PASSES):
-                n = c * PASSES + g
-                nc.tensor.matmul_mx(
-                    out=acc,
-                    lhsT=w_codes[which][:, n, features].bitcast(FP8X4),
-                    lhsT_scale=w_planes[which][PLANE_ROWS * n : P, features],
-                    rhs=h_codes[:, g, tokens].bitcast(FP8X4),
-                    rhs_scale=h_planes[:, g, tokens],
-                    start=(g == 0),
-                    stop=(g == PASSES - 1),
-                )
-
-        def side_by_side(rows, s):
-            grouped = work.tile([P, TOKENS, PACK], BF16, name="k_grouped", bufs=4, align_bytes=64)
-            nc.vector.tensor_copy(
-                out=grouped[:].rearrange("p (n i) t -> p n t i", i=4),
-                in_=rows[:, s, :, :].rearrange("p t (n i) -> p n t i", i=4),
-            )
-            return grouped
-
-        def quantise_keys(grouped, codes, planes, s):
-            nc.vector.quantize_mx(
-                out=codes[:, s, :].bitcast(FP8X4),
-                scales=planes[:, s, :],
-                in_=grouped[:].rearrange("p r t -> p (r t)"),
+            grouped, codes, planes = tiles_of[(i, "k")]
+            cols = slice(u * P, (u + 1) * P)
+            project("k", b, c, u, s, grouped[:, s, cols, :])
+            return lambda: nc.vector.quantize_mx(
+                out=codes[:, s, cols].bitcast(FP8X4),
+                scales=planes[:, s, cols],
+                in_=grouped[:, s, cols, :].rearrange("p r t -> p (r t)"),
             )
 
-        def new_codes(b, c, name):
-            tiles_of[(b, c, name)] = (
-                work.tile([P, PASSES, TOKENS], U32, name=name + "_codes", align_bytes=64),
-                work.tile([P, PASSES, TOKENS], U8, name=name + "_planes", align_bytes=64),
+        def query_unit(i, u, s):
+            b, c = pairs[i]
+            if (u, s) == (0, 0):
+                tiles_of[(i, "q")] = (
+                    work.tile([P, TOKEN_TILES, PASSES, P, PACK], BF16, name="q_grouped", align_bytes=64),
+                    work.tile([P, TOKEN_TILES, PASSES, P], U32, name="q_codes", align_bytes=64),
+                    work.tile([P, TOKEN_TILES, PASSES, P], U8, name="q_planes", align_bytes=64),
+                )
+            grouped, codes, planes = tiles_of[(i, "q")]
+            project("q", b, c, u, s, grouped[:, u, s, :, :])
+            return lambda: nc.vector.quantize_mx(
+                out=codes[:, u, s, :].bitcast(FP8X4),
+                scales=planes[:, u, s, :],
+                in_=grouped[:, u, s, :, :].rearrange("p r t -> p (r t)"),
             )
 
-        def project_keys(b, c):
-            rows = work.tile([P, PASSES, PACK, TOKENS], BF16, name="k_rows")
-            moved = work.tile([P, PASSES, PACK, TOKENS], BF16, name="k_moved")
-            tiles_of[(b, c, "rows")] = rows
-            tiles_of[(b, c, "moved")] = moved
-            for s in range(PASSES):
-                for t in range(PACK):
-                    acc = psum.tile([P, TOKENS], F32, name="proj", bufs=PROJ_BANKS)
-                    project_tile(acc[:], "k", c, s * PACK + t, slice(b * TOKENS, (b + 1) * TOKENS))
-                    nc.scalar.copy(out=rows[:, s, t, :], in_=acc[:])
-                    nc.sync.dma_start(
-                        out=moved[QUARTER * t : QUARTER * (t + 1), s, :, :], in_=rows[:, s, t, :]
-                    )
-
-        def quantise_key_copy(b, c, source, name):
-            new_codes(b, c, name)
-            codes, planes = tiles_of[(b, c, name)]
-            grouped = [side_by_side(tiles_of[(b, c, source)], s) for s in range(PASSES)]
-            for s in range(PASSES):
-                quantise_keys(grouped[s], codes, planes, s)
-
-        def project_queries(b, c, ahead):
-            if ahead is not None:
-                new_codes(ahead[0], ahead[1], "k_tile")
-                k_codes, k_planes = tiles_of[(ahead[0], ahead[1], "k_tile")]
-                k_rows = tiles_of[(ahead[0], ahead[1], "rows")]
-                k_grouped = []
-            codes = work.tile([P, TOKEN_TILES, PASSES, P], U32, name="q_codes", align_bytes=64)
-            planes = work.tile([P, TOKEN_TILES, PASSES, P], U8, name="q_planes", align_bytes=64)
-            tiles_of[(b, c, "q")] = (codes, planes)
-            for u in range(TOKEN_TILES):
-                first = b * TOKENS + u * P
-                grouped = work.tile([P, PASSES, P, PACK], BF16, name="q_grouped", bufs=4, align_bytes=64)
-                for s in range(PASSES):
-                    acc = psum.tile([P, PACK, P], F32, name="q_proj", tag="proj", bufs=PROJ_BANKS)
-                    for t in range(PACK):
-                        project_tile(acc[:, t, :], "q", c, s * PACK + t, slice(first, first + P))
-                    nc.scalar.copy(out=grouped[:, s, :, :], in_=acc[:].rearrange("p t r -> p r t"))
-                if ahead is not None and u < PASSES:
-                    k_grouped.append(side_by_side(k_rows, u))
-                elif ahead is not None:
-                    quantise_keys(k_grouped[u - PASSES], k_codes, k_planes, u - PASSES)
-                nc.vector.quantize_mx(
-                    out=codes[:, u, :, :].rearrange("p s r -> p (s r)").bitcast(FP8X4),
-                    scales=planes[:, u, :, :].rearrange("p s r -> p (s r)"),
-                    in_=grouped[:].rearrange("p s r t -> p (s r t)"),
-                )
-
-        def score_tile(b, c, first_row, rows_of_pass, keys):
-            k_codes, k_planes = keys
+        def score_tile(i, first_row):
+            b, c = pairs[i]
+            grouped, k_codes, k_planes = tiles_of[(i, "k")]
+            q_grouped, q_codes, q_planes = tiles_of[(i, "q")]
             acc = psum.tile([P, TOKENS], F32, name="score", bufs=SCORE_BANKS)
             for s in range(PASSES):
-                rows, rows_scale = rows_of_pass(s)
+                if first_row == TOKENS:
+                    n = c * PASSES + s
+                    rows, rows_scale = emb_codes[:, n, :], emb_planes[PLANE_ROWS * n : P, :]
+                else:
+                    u = first_row // P
+                    rows, rows_scale = q_codes[:, u, s, :], q_planes[:, u, s, :]
                 nc.tensor.matmul_mx(
                     out=acc[:],
                     lhsT=rows.bitcast(FP8X4),
@@ -237,45 +231,70 @@ def tile_relationtagger_pa_e_kernel(
                     start=(s == 0),
                     stop=(s == PASSES - 1),
                 )
-            gated = work.tile([P, TOKENS], F32, name="gated", bufs=6)
-            nc.vector.tensor_tensor(out=gated[:], in0=acc[:], in1=gate[:, c, b, :], op=mybir.AluOpType.mult)
-            nc.sync.dma_start(out=out[b, c, first_row : first_row + P, :], in_=gated[:])
 
-        def score(b, c):
-            score_tile(
-                b,
-                c,
-                TOKENS,
-                lambda s: (emb_codes[:, c * PASSES + s, :], emb_planes[PLANE_ROWS * (c * PASSES + s) : P, :]),
-                tiles_of[(b, c, "k_packed")],
-            )
-            q_codes, q_planes = tiles_of[(b, c, "q")]
-            for u in range(TOKEN_TILES):
-                score_tile(
-                    b, c, u * P, lambda s: (q_codes[:, u, s, :], q_planes[:, u, s, :]), tiles_of[(b, c, "k_tile")]
-                )
+            def gate_and_store():
+                gated = work.tile([P, TOKENS], F32, name="gated", bufs=6)
+                nc.vector.tensor_tensor(out=gated[:], in0=acc[:], in1=gate[:, c, b, :], op=mybir.AluOpType.mult)
+                nc.sync.dma_start(out=out[b, c, first_row : first_row + P, :], in_=gated[:])
+
+            return gate_and_store
 
         pairs = [(b, c) for b in range(BATCH) for c in range(CHANNELS)]
+        pending = []
 
-        def pair_at(i):
-            return pairs[i] if i < len(pairs) else None
+        def step(*results):
+            for task in pending:
+                task()
+            pending.clear()
+            pending.extend(results)
 
-        load_what_the_first_steps_need()
-        flip_hidden(0)
-        quantise_hidden(0)
-        spread_gate()
-        project_keys(*pairs[0])
-        load_the_rest()
-        quantise_key_copy(*pairs[0], "rows", "k_tile")
-        for i, (b, c) in enumerate(pairs):
-            ahead = pair_at(i + 1)
-            new_batch = pair_at(i + 2) is not None and pair_at(i + 2)[1] == 0
-            if ahead is not None:
-                project_keys(*ahead)
-            quantise_key_copy(b, c, "moved", "k_packed")
-            if new_batch:
-                flip_hidden(pair_at(i + 2)[0])
-            project_queries(b, c, ahead)
-            if new_batch:
-                quantise_hidden(pair_at(i + 2)[0])
-            score(b, c)
+        load_all()
+        flip_hidden(0, 0)
+        sort_planes("k", 0)
+        sort_words("k", 0, 0, 0)
+        sort_words("k", 0, 0, 1)
+        quantise_hidden(0, 0)
+        flip_hidden(0, 1)
+        sort_planes("k", 1)
+        sort_words("k", 0, 1, 0)
+        sort_words("k", 0, 1, 1)
+        quantise_hidden(0, 1)
+
+        label_row = TOKENS
+        also = {
+            (0, 1): [lambda: flip_hidden(0, 2), lambda: quantise_hidden(0, 2)],
+            (0, 3): [lambda: flip_hidden(0, 3), lambda: quantise_hidden(0, 3), lambda: sort_planes("q", 0)],
+            (0, 4): [lambda: sort_planes("q", 1)],
+            (0, 5): [lambda: sort_words("q", 0, 0, 0), lambda: sort_words("q", 0, 0, 1)],
+            (0, 6): [lambda: sort_words("q", 0, 1, 0), lambda: sort_words("q", 0, 1, 1)],
+            (0, 11): [lambda: sort_words("k", 1, 0, 0)],
+            (0, 12): [lambda: sort_words("k", 1, 0, 1)],
+            (0, 13): [lambda: sort_words("k", 1, 1, 0)],
+            (0, 14): [lambda: sort_words("k", 1, 1, 1)],
+            (1, 1): [lambda: sort_words("q", 1, 0, 0)],
+            (1, 2): [lambda: sort_words("q", 1, 0, 1)],
+            (1, 4): [lambda: sort_words("q", 1, 1, 0)],
+            (1, 5): [lambda: sort_words("q", 1, 1, 1)],
+            (1, 7): [lambda: flip_hidden(1, 0), lambda: flip_hidden(1, 1)],
+            (1, 8): [lambda: quantise_hidden(1, 0), lambda: quantise_hidden(1, 1)],
+            (1, 10): [lambda: flip_hidden(1, 2), lambda: flip_hidden(1, 3)],
+            (1, 11): [lambda: quantise_hidden(1, 2), lambda: quantise_hidden(1, 3)],
+        }
+        scores_before = {2: label_row, 5: 0, 8: P, 11: 2 * P, 14: 3 * P}
+        last_scores_before = {1: label_row, 2: 0, 4: P, 5: 2 * P, 7: 3 * P}
+        last_scores = {11: label_row, 13: 0, 15: P}
+        last = len(pairs) - 1
+        for i in range(len(pairs)):
+            for j in range(2 * UNITS):
+                u, s = (j % UNITS) // PASSES, j % PASSES
+                step((key_unit if j < UNITS else query_unit)(i, u, s))
+                for task in also.get((i, j), []):
+                    task()
+                before = last_scores_before if i == last else scores_before
+                if i > 0 and j in before:
+                    step(score_tile(i - 1, before[j]))
+                if i == last and j in last_scores:
+                    step(score_tile(i, last_scores[j]))
+        step(score_tile(last, 2 * P))
+        step(score_tile(last, 3 * P))
+        step()

@@ -22,7 +22,6 @@ K_PASS = P * PACK
 PASSES = WIDTH // K_PASS
 TOKEN_TILES = TOKENS // P
 PLANE_ROWS = 4
-UNITS = TOKEN_TILES * PASSES
 
 PROJ_BANKS = 5
 SCORE_BANKS = 3
@@ -157,58 +156,61 @@ def tile_relationtagger_pa_e_kernel(
                     in_=h_grouped[(b, u)][:, g, :, :].rearrange("p s t -> p (s t)"),
                 )
 
-        def project(which, b, c, u, s, grouped):
-            tokens = slice(b * TOKENS + u * P, b * TOKENS + (u + 1) * P)
-            acc = psum.tile([P, PACK, P], F32, name="proj", bufs=PROJ_BANKS)
-            for t in range(PACK):
-                features = slice(s * K_PASS + t * P, s * K_PASS + (t + 1) * P)
-                for g in range(PASSES):
-                    n = c * PASSES + g
-                    nc.tensor.matmul_mx(
-                        out=acc[:, t, :],
-                        lhsT=w_codes[which][:, n, features].bitcast(FP8X4),
-                        lhsT_scale=w_planes[which][PLANE_ROWS * n : P, features],
-                        rhs=h_codes[:, g, tokens].bitcast(FP8X4),
-                        rhs_scale=h_planes[:, g, tokens],
-                        start=(g == 0),
-                        stop=(g == PASSES - 1),
-                    )
-            nc.scalar.copy(out=grouped, in_=acc[:].rearrange("p t r -> p r t"))
-
         tiles_of = {}
 
-        def key_unit(i, u, s):
+        def project(i, which, first, count, s):
             b, c = pairs[i]
-            if (u, s) == (0, 0):
-                tiles_of[(i, "k")] = (
-                    work.tile([P, PASSES, TOKENS, PACK], BF16, name="k_grouped", align_bytes=64),
-                    work.tile([P, PASSES, TOKENS], U32, name="k_codes", align_bytes=64),
-                    work.tile([P, PASSES, TOKENS], U8, name="k_planes", align_bytes=64),
+            if (i, which) not in tiles_of:
+                tiles_of[(i, which)] = (
+                    work.tile([P, PASSES, TOKENS, PACK], BF16, name=which + "_grouped", align_bytes=64),
+                    work.tile([P, PASSES, TOKENS], U32, name=which + "_codes", align_bytes=64),
+                    work.tile([P, PASSES, TOKENS], U8, name=which + "_planes", align_bytes=64),
                 )
-            grouped, codes, planes = tiles_of[(i, "k")]
-            cols = slice(u * P, (u + 1) * P)
-            project("k", b, c, u, s, grouped[:, s, cols, :])
-            return lambda: nc.vector.quantize_mx(
-                out=codes[:, s, cols].bitcast(FP8X4),
-                scales=planes[:, s, cols],
-                in_=grouped[:, s, cols, :].rearrange("p r t -> p (r t)"),
-            )
+            grouped, codes, planes = tiles_of[(i, which)]
+            tokens = slice(b * TOKENS + first, b * TOKENS + first + count)
+            cols = slice(first, first + count)
+            per_bank = TOKENS // count
 
-        def query_unit(i, u, s):
-            b, c = pairs[i]
-            if (u, s) == (0, 0):
-                tiles_of[(i, "q")] = (
-                    work.tile([P, TOKEN_TILES, PASSES, P, PACK], BF16, name="q_grouped", align_bytes=64),
-                    work.tile([P, TOKEN_TILES, PASSES, P], U32, name="q_codes", align_bytes=64),
-                    work.tile([P, TOKEN_TILES, PASSES, P], U8, name="q_planes", align_bytes=64),
+            def bank(h):
+                acc = psum.tile([P, per_bank, count], F32, name="proj", bufs=PROJ_BANKS)
+                for e in range(per_bank):
+                    t = per_bank * h + e
+                    features = slice(s * K_PASS + t * P, s * K_PASS + (t + 1) * P)
+                    for g in range(PASSES):
+                        n = c * PASSES + g
+                        nc.tensor.matmul_mx(
+                            out=acc[:, e, :],
+                            lhsT=w_codes[which][:, n, features].bitcast(FP8X4),
+                            lhsT_scale=w_planes[which][PLANE_ROWS * n : P, features],
+                            rhs=h_codes[:, g, tokens].bitcast(FP8X4),
+                            rhs_scale=h_planes[:, g, tokens],
+                            start=(g == 0),
+                            stop=(g == PASSES - 1),
+                        )
+                return acc[:].rearrange("p e r -> p r e")
+
+            def quantise():
+                nc.vector.quantize_mx(
+                    out=codes[:, s, cols].bitcast(FP8X4),
+                    scales=planes[:, s, cols],
+                    in_=grouped[:, s, cols, :].rearrange("p r t -> p (r t)"),
                 )
-            grouped, codes, planes = tiles_of[(i, "q")]
-            project("q", b, c, u, s, grouped[:, u, s, :, :])
-            return lambda: nc.vector.quantize_mx(
-                out=codes[:, u, s, :].bitcast(FP8X4),
-                scales=planes[:, u, s, :],
-                in_=grouped[:, u, s, :, :].rearrange("p r t -> p (r t)"),
-            )
+
+            if per_bank == PACK:
+                nc.scalar.copy(out=grouped[:, s, cols, :], in_=bank(0))
+                return [quantise]
+
+            halves = work.tile([P, 2, count, 2], BF16, name="halves", bufs=4, align_bytes=64)
+            for h in range(2):
+                nc.scalar.copy(out=halves[:, h, :, :], in_=bank(h))
+
+            def join():
+                nc.vector.tensor_copy(
+                    out=grouped[:, s, cols, :].rearrange("p r t -> p (r t)").bitcast(F32).rearrange("p (r h) -> p r h", h=2),
+                    in_=halves[:].rearrange("p h r e -> p (h r e)").bitcast(F32).rearrange("p (h r) -> p r h", h=2),
+                )
+
+            return [join, quantise]
 
         def score_tile(i, first_row):
             b, c = pairs[i]
@@ -220,8 +222,7 @@ def tile_relationtagger_pa_e_kernel(
                     n = c * PASSES + s
                     rows, rows_scale = emb_codes[:, n, :], emb_planes[PLANE_ROWS * n : P, :]
                 else:
-                    u = first_row // P
-                    rows, rows_scale = q_codes[:, u, s, :], q_planes[:, u, s, :]
+                    rows, rows_scale = q_codes[:, s, first_row : first_row + P], q_planes[:, s, first_row : first_row + P]
                 nc.tensor.matmul_mx(
                     out=acc[:],
                     lhsT=rows.bitcast(FP8X4),
@@ -237,16 +238,16 @@ def tile_relationtagger_pa_e_kernel(
                 nc.vector.tensor_tensor(out=gated[:], in0=acc[:], in1=gate[:, c, b, :], op=mybir.AluOpType.mult)
                 nc.sync.dma_start(out=out[b, c, first_row : first_row + P, :], in_=gated[:])
 
-            return gate_and_store
+            return [gate_and_store]
 
         pairs = [(b, c) for b in range(BATCH) for c in range(CHANNELS)]
-        pending = []
+        made = []
 
-        def step(*results):
-            for task in pending:
-                task()
-            pending.clear()
-            pending.extend(results)
+        def step(tasks):
+            made.append(tasks)
+            for lag in (1, 2):
+                if len(made) > lag and len(made[-1 - lag]) >= lag:
+                    made[-1 - lag][lag - 1]()
 
         load_all()
         flip_hidden(0, 0)
@@ -261,40 +262,50 @@ def tile_relationtagger_pa_e_kernel(
         quantise_hidden(0, 1)
 
         label_row = TOKENS
+        narrow = [(u * P, P) for u in range(TOKEN_TILES)]
+        wide = [(0, 2 * P), (2 * P, 2 * P)]
+        mixed = [(0, 2 * P), (2 * P, P), (3 * P, P)]
+
+        def units_of(which, pieces):
+            return [(which, first, count, s) for first, count in pieces for s in range(PASSES)]
+
+        units = [
+            units_of("k", narrow) + units_of("q", wide),
+            units_of("k", wide) + units_of("q", wide),
+            units_of("k", wide) + units_of("q", wide),
+            units_of("k", wide) + units_of("q", mixed),
+        ]
         also = {
             (0, 1): [lambda: flip_hidden(0, 2), lambda: quantise_hidden(0, 2)],
             (0, 3): [lambda: flip_hidden(0, 3), lambda: quantise_hidden(0, 3), lambda: sort_planes("q", 0)],
             (0, 4): [lambda: sort_planes("q", 1)],
             (0, 5): [lambda: sort_words("q", 0, 0, 0), lambda: sort_words("q", 0, 0, 1)],
             (0, 6): [lambda: sort_words("q", 0, 1, 0), lambda: sort_words("q", 0, 1, 1)],
-            (0, 11): [lambda: sort_words("k", 1, 0, 0)],
-            (0, 12): [lambda: sort_words("k", 1, 0, 1)],
-            (0, 13): [lambda: sort_words("k", 1, 1, 0)],
-            (0, 14): [lambda: sort_words("k", 1, 1, 1)],
-            (1, 1): [lambda: sort_words("q", 1, 0, 0)],
-            (1, 2): [lambda: sort_words("q", 1, 0, 1)],
-            (1, 4): [lambda: sort_words("q", 1, 1, 0)],
-            (1, 5): [lambda: sort_words("q", 1, 1, 1)],
-            (1, 7): [lambda: flip_hidden(1, 0), lambda: flip_hidden(1, 1)],
-            (1, 8): [lambda: quantise_hidden(1, 0), lambda: quantise_hidden(1, 1)],
-            (1, 10): [lambda: flip_hidden(1, 2), lambda: flip_hidden(1, 3)],
-            (1, 11): [lambda: quantise_hidden(1, 2), lambda: quantise_hidden(1, 3)],
+            (0, 9): [lambda: sort_words("k", 1, 0, 0), lambda: sort_words("k", 1, 0, 1)],
+            (0, 10): [lambda: sort_words("k", 1, 1, 0), lambda: sort_words("k", 1, 1, 1)],
+            (1, 0): [lambda: sort_words("q", 1, 0, 0), lambda: sort_words("q", 1, 0, 1)],
+            (1, 2): [lambda: sort_words("q", 1, 1, 0), lambda: sort_words("q", 1, 1, 1)],
+            (1, 3): [lambda: flip_hidden(1, 0), lambda: flip_hidden(1, 1)],
+            (1, 4): [lambda: quantise_hidden(1, 0), lambda: quantise_hidden(1, 1)],
+            (1, 5): [lambda: flip_hidden(1, 2), lambda: flip_hidden(1, 3)],
+            (1, 6): [lambda: quantise_hidden(1, 2), lambda: quantise_hidden(1, 3)],
         }
-        scores_before = {2: label_row, 5: 0, 8: P, 11: 2 * P, 14: 3 * P}
-        last_scores_before = {1: label_row, 2: 0, 4: P, 5: 2 * P, 7: 3 * P}
-        last_scores = {11: label_row, 13: 0, 15: P}
+        rows_in_turn = [label_row, 0, P, 2 * P, 3 * P]
         last = len(pairs) - 1
+        scores = {}
+        for i in range(1, last):
+            for j, row in zip([1, 2, 4, 5, 7], rows_in_turn):
+                scores[(i, j)] = [(i - 1, row)]
+        for j, row in zip([0, 1, 2, 3, 4], rows_in_turn):
+            scores[(last, j)] = [(last - 1, row)]
+        scores[(last, 6)] = [(last, label_row)]
+        scores[(last, 7)] = [(last, 0)]
+        scores[(last, 9)] = [(last, P), (last, 2 * P), (last, 3 * P)]
         for i in range(len(pairs)):
-            for j in range(2 * UNITS):
-                u, s = (j % UNITS) // PASSES, j % PASSES
-                step((key_unit if j < UNITS else query_unit)(i, u, s))
+            for j, unit in enumerate(units[i]):
+                step(project(i, *unit))
                 for task in also.get((i, j), []):
                     task()
-                before = last_scores_before if i == last else scores_before
-                if i > 0 and j in before:
-                    step(score_tile(i - 1, before[j]))
-                if i == last and j in last_scores:
-                    step(score_tile(i, last_scores[j]))
-        step(score_tile(last, 2 * P))
-        step(score_tile(last, 3 * P))
-        step()
+                for of_pair, row in scores.get((i, j), []):
+                    step(score_tile(of_pair, row))
+        step([])

@@ -63,6 +63,8 @@ def tile_relationtagger_pa_e_kernel(
         h_planes = keep.tile([P, PASSES, BATCH * TOKENS], U8, align_bytes=64)
         ident_f32 = keep.tile([P, P], F32)
 
+        still = keep.tile([P, TOKENS], BF16)
+        nc.gpsimd.memset(still[:].bitcast(F32), 0.0)
         make_identity(nc, ident_f32[:])
         for planes in (raw_planes["k"], raw_planes["q"], emb_planes):
             nc.vector.memset(planes[:].bitcast(I32), 0)
@@ -90,11 +92,11 @@ def tile_relationtagger_pa_e_kernel(
         def load_all():
             load_hidden(0, 0)
             load_planes(raw_planes["k"], Wk_scales)
-            load_weight("k", Wk_words, 0, 0)
             load_hidden(0, 1)
-            load_weight("k", Wk_words, 0, 1)
+            load_weight("k", Wk_words, 0, 0)
             load_hidden(0, 2)
             load_hidden(0, 3)
+            load_weight("k", Wk_words, 0, 1)
             load_planes(raw_planes["q"], Wq_scales)
             load_weight("q", Wq_words, 0, 0)
             load_weight("q", Wq_words, 0, 1)
@@ -128,6 +130,11 @@ def tile_relationtagger_pa_e_kernel(
                 out=w_codes[which][:, n, cols].bitcast(I32).rearrange("p (t n i) -> p n t i", t=PACK, i=4),
                 in_=raw_codes[which][:, n, cols].bitcast(I32).rearrange("p (n i t) -> p n t i", t=PACK, i=4),
             )
+
+        def keep_awake(count):
+            for turn in range(count):
+                idle = psum.tile([P, TOKENS], F32, name="idle", tag="score", bufs=SCORE_BANKS)
+                nc.tensor.matmul(out=idle[:], lhsT=still[:, :P], rhs=still[:], start=True, stop=True)
 
         h_grouped = {}
 
@@ -250,39 +257,43 @@ def tile_relationtagger_pa_e_kernel(
                     made[-1 - lag][lag - 1]()
 
         load_all()
+        keep_awake(4)
         flip_hidden(0, 0)
+        flip_hidden(0, 1)
+        keep_awake(2)
         sort_planes("k", 0)
+        quantise_hidden(0, 0)
         sort_words("k", 0, 0, 0)
         sort_words("k", 0, 0, 1)
-        quantise_hidden(0, 0)
-        flip_hidden(0, 1)
-        sort_planes("k", 1)
-        sort_words("k", 0, 1, 0)
-        sort_words("k", 0, 1, 1)
         quantise_hidden(0, 1)
 
         label_row = TOKENS
-        narrow = [(u * P, P) for u in range(TOKEN_TILES)]
         wide = [(0, 2 * P), (2 * P, 2 * P)]
         mixed = [(0, 2 * P), (2 * P, P), (3 * P, P)]
 
         def units_of(which, pieces):
             return [(which, first, count, s) for first, count in pieces for s in range(PASSES)]
 
+        first_keys = [("k", 0, P, 0), ("k", P, P, 0), ("k", 0, 2 * P, 1)] + units_of("k", wide[1:])
         units = [
-            units_of("k", narrow) + units_of("q", wide),
+            first_keys + units_of("q", wide),
             units_of("k", wide) + units_of("q", wide),
             units_of("k", wide) + units_of("q", wide),
             units_of("k", wide) + units_of("q", mixed),
         ]
         also = {
-            (0, 1): [lambda: flip_hidden(0, 2), lambda: quantise_hidden(0, 2)],
-            (0, 3): [lambda: flip_hidden(0, 3), lambda: quantise_hidden(0, 3), lambda: sort_planes("q", 0)],
-            (0, 4): [lambda: sort_planes("q", 1)],
-            (0, 5): [lambda: sort_words("q", 0, 0, 0), lambda: sort_words("q", 0, 0, 1)],
-            (0, 6): [lambda: sort_words("q", 0, 1, 0), lambda: sort_words("q", 0, 1, 1)],
-            (0, 9): [lambda: sort_words("k", 1, 0, 0), lambda: sort_words("k", 1, 0, 1)],
-            (0, 10): [lambda: sort_words("k", 1, 1, 0), lambda: sort_words("k", 1, 1, 1)],
+            (0, 1): [
+                lambda: flip_hidden(0, 2),
+                lambda: flip_hidden(0, 3),
+                lambda: sort_planes("k", 1),
+                lambda: sort_words("k", 0, 1, 0),
+                lambda: sort_words("k", 0, 1, 1),
+            ],
+            (0, 2): [lambda: quantise_hidden(0, 2), lambda: quantise_hidden(0, 3), lambda: sort_planes("q", 0)],
+            (0, 3): [lambda: sort_words("q", 0, 0, 0), lambda: sort_words("q", 0, 0, 1), lambda: sort_planes("q", 1)],
+            (0, 4): [lambda: sort_words("q", 0, 1, 0), lambda: sort_words("q", 0, 1, 1)],
+            (0, 6): [lambda: sort_words("k", 1, 0, 0), lambda: sort_words("k", 1, 0, 1)],
+            (0, 7): [lambda: sort_words("k", 1, 1, 0), lambda: sort_words("k", 1, 1, 1)],
             (1, 0): [lambda: sort_words("q", 1, 0, 0), lambda: sort_words("q", 1, 0, 1)],
             (1, 2): [lambda: sort_words("q", 1, 1, 0), lambda: sort_words("q", 1, 1, 1)],
             (1, 3): [lambda: flip_hidden(1, 0), lambda: flip_hidden(1, 1)],

@@ -59,12 +59,16 @@ def tile_relationtagger_pa_e_kernel(
         }
         emb_planes = keep.tile([P, LABELS], U8, align_bytes=64)
         gate = keep.tile([P, CHANNELS, BATCH, TOKENS], BF16)
+        gate_row = keep.tile([P, TOKENS], BF16)
+        ones = keep.tile([P, P], BF16)
         h_codes = keep.tile([P, PASSES, BATCH * TOKENS], U32, align_bytes=64)
         h_planes = keep.tile([P, PASSES, BATCH * TOKENS], U8, align_bytes=64)
         ident_f32 = keep.tile([P, P], F32)
 
         still = keep.tile([P, TOKENS], BF16)
         nc.gpsimd.memset(still[:].bitcast(F32), 0.0)
+        nc.gpsimd.memset(gate_row[:].bitcast(F32), 0.0)
+        nc.gpsimd.memset(ones[:], 1.0)
         make_identity(nc, ident_f32[:])
         for planes in (raw_planes["k"], raw_planes["q"], emb_planes):
             nc.vector.memset(planes[:].bitcast(I32), 0)
@@ -81,18 +85,18 @@ def tile_relationtagger_pa_e_kernel(
             nc.sync.dma_start(out=hidden_sb[:, b, u, :], in_=hidden[b, u * P : (u + 1) * P, :])
 
         def load_weight(which, words, c, s):
-            for g in range(PASSES):
-                n = c * PASSES + g
-                cols = slice(s * K_PASS, (s + 1) * K_PASS)
-                nc.sync.dma_start(
-                    out=raw_codes[which][:, n, cols].bitcast(I32),
-                    in_=words[n].rearrange("p n t -> p (n t)").bitcast(I32)[:, cols],
-                )
+            both = slice(c * PASSES, (c + 1) * PASSES)
+            cols = slice(s * K_PASS, (s + 1) * K_PASS)
+            nc.sync.dma_start(
+                out=raw_codes[which][:, both, cols].bitcast(I32),
+                in_=words[both].rearrange("g p n t -> p g (n t)").bitcast(I32)[:, :, cols],
+            )
 
         def load_all():
             load_hidden(0, 0)
             load_planes(raw_planes["k"], Wk_scales)
             load_hidden(0, 1)
+            nc.sync.dma_start(out=gate_row[0:1], in_=vsum[0, 0:1, :])
             load_weight("k", Wk_words, 0, 0)
             load_hidden(0, 2)
             load_hidden(0, 3)
@@ -102,10 +106,6 @@ def tile_relationtagger_pa_e_kernel(
             load_weight("q", Wq_words, 0, 1)
             load_weight("k", Wk_words, 1, 0)
             load_weight("k", Wk_words, 1, 1)
-            nc.sync.dma_start(
-                out=gate[:].rearrange("p c b t -> p (c b t)"),
-                in_=vsum.rearrange("c b t -> (c b t)").partition_broadcast(P),
-            )
             load_planes(emb_planes, emb_scales)
             nc.sync.dma_start(
                 out=emb_codes[:].bitcast(I32),
@@ -115,6 +115,8 @@ def tile_relationtagger_pa_e_kernel(
                 load_hidden(1, u)
             load_weight("q", Wq_words, 1, 0)
             load_weight("q", Wq_words, 1, 1)
+            for b, c in pairs[1:]:
+                nc.sync.dma_start(out=gate[:, c, b, :], in_=vsum[c, b, :].partition_broadcast(P))
 
         def sort_planes(which, s):
             cols = slice(s * K_PASS, (s + 1) * K_PASS)
@@ -135,6 +137,12 @@ def tile_relationtagger_pa_e_kernel(
             for turn in range(count):
                 idle = psum.tile([P, TOKENS], F32, name="idle", tag="score", bufs=SCORE_BANKS)
                 nc.tensor.matmul(out=idle[:], lhsT=still[:, :P], rhs=still[:], start=True, stop=True)
+
+        def spread_first_gate():
+            b, c = pairs[0]
+            spread = psum.tile([P, TOKENS], F32, name="spread", tag="score", bufs=SCORE_BANKS)
+            nc.tensor.matmul(out=spread[:], lhsT=ones[:], rhs=gate_row[:], start=True, stop=True)
+            nc.scalar.copy(out=gate[:, c, b, :], in_=spread[:])
 
         h_grouped = {}
 
@@ -260,8 +268,10 @@ def tile_relationtagger_pa_e_kernel(
         keep_awake(4)
         flip_hidden(0, 0)
         flip_hidden(0, 1)
-        keep_awake(2)
+        keep_awake(1)
+        spread_first_gate()
         sort_planes("k", 0)
+        sort_planes("k", 1)
         quantise_hidden(0, 0)
         sort_words("k", 0, 0, 0)
         sort_words("k", 0, 0, 1)
@@ -285,15 +295,20 @@ def tile_relationtagger_pa_e_kernel(
             (0, 1): [
                 lambda: flip_hidden(0, 2),
                 lambda: flip_hidden(0, 3),
-                lambda: sort_planes("k", 1),
                 lambda: sort_words("k", 0, 1, 0),
                 lambda: sort_words("k", 0, 1, 1),
             ],
-            (0, 2): [lambda: quantise_hidden(0, 2), lambda: quantise_hidden(0, 3), lambda: sort_planes("q", 0)],
-            (0, 3): [lambda: sort_words("q", 0, 0, 0), lambda: sort_words("q", 0, 0, 1), lambda: sort_planes("q", 1)],
-            (0, 4): [lambda: sort_words("q", 0, 1, 0), lambda: sort_words("q", 0, 1, 1)],
-            (0, 6): [lambda: sort_words("k", 1, 0, 0), lambda: sort_words("k", 1, 0, 1)],
-            (0, 7): [lambda: sort_words("k", 1, 1, 0), lambda: sort_words("k", 1, 1, 1)],
+            (0, 2): [
+                lambda: quantise_hidden(0, 2),
+                lambda: quantise_hidden(0, 3),
+                lambda: sort_planes("q", 0),
+                lambda: sort_planes("q", 1),
+                lambda: sort_words("q", 0, 0, 0),
+                lambda: sort_words("q", 0, 0, 1),
+            ],
+            (0, 3): [lambda: sort_words("q", 0, 1, 0), lambda: sort_words("q", 0, 1, 1)],
+            (0, 5): [lambda: sort_words("k", 1, 0, 0), lambda: sort_words("k", 1, 0, 1)],
+            (0, 6): [lambda: sort_words("k", 1, 1, 0), lambda: sort_words("k", 1, 1, 1)],
             (1, 0): [lambda: sort_words("q", 1, 0, 0), lambda: sort_words("q", 1, 0, 1)],
             (1, 2): [lambda: sort_words("q", 1, 1, 0), lambda: sort_words("q", 1, 1, 1)],
             (1, 3): [lambda: flip_hidden(1, 0), lambda: flip_hidden(1, 1)],

@@ -41,8 +41,8 @@ def tile_relationtagger_pa_e_kernel(
 
         hidden_sb = keep.tile([P, BATCH, TOKEN_TILES, WIDTH], BF16)
         raw_codes = {
-            "k": keep.tile([P, CHANNELS * PASSES, WIDTH], U32, name="wk_raw", align_bytes=64),
-            "q": keep.tile([P, CHANNELS * PASSES, WIDTH], U32, name="wq_raw", align_bytes=64),
+            "k": keep.tile([P, CHANNELS, PASSES, PASSES, K_PASS], U32, name="wk_raw", align_bytes=64),
+            "q": keep.tile([P, CHANNELS, PASSES, PASSES, K_PASS], U32, name="wq_raw", align_bytes=64),
         }
         w_codes = {
             "k": keep.tile([P, CHANNELS * PASSES, WIDTH], U32, name="wk_codes", align_bytes=64),
@@ -85,19 +85,19 @@ def tile_relationtagger_pa_e_kernel(
             nc.sync.dma_start(out=hidden_sb[:, b, u, :], in_=hidden[b, u * P : (u + 1) * P, :])
 
         def load_weight(which, words, c, s):
-            both = slice(c * PASSES, (c + 1) * PASSES)
             cols = slice(s * K_PASS, (s + 1) * K_PASS)
-            nc.sync.dma_start(
-                out=raw_codes[which][:, both, cols].bitcast(I32),
-                in_=words[both].rearrange("g p n t -> p g (n t)").bitcast(I32)[:, :, cols],
-            )
+            for g in range(PASSES):
+                nc.sync.dma_start(
+                    out=raw_codes[which][:, c, s, g, :].bitcast(I32),
+                    in_=words[c * PASSES + g].rearrange("p n t -> p (n t)").bitcast(I32)[:, cols],
+                )
 
         def load_all():
             load_hidden(0, 0)
             load_planes(raw_planes["k"], Wk_scales)
             load_hidden(0, 1)
-            nc.sync.dma_start(out=gate_row[0:1], in_=vsum[0, 0:1, :])
             load_weight("k", Wk_words, 0, 0)
+            nc.sync.dma_start(out=gate_row[0:1], in_=vsum[0, 0:1, :])
             load_hidden(0, 2)
             load_hidden(0, 3)
             load_weight("k", Wk_words, 0, 1)
@@ -130,7 +130,7 @@ def tile_relationtagger_pa_e_kernel(
             cols = slice(s * K_PASS, (s + 1) * K_PASS)
             nc.vector.tensor_copy(
                 out=w_codes[which][:, n, cols].bitcast(I32).rearrange("p (t n i) -> p n t i", t=PACK, i=4),
-                in_=raw_codes[which][:, n, cols].bitcast(I32).rearrange("p (n i t) -> p n t i", t=PACK, i=4),
+                in_=raw_codes[which][:, c, s, g, :].bitcast(I32).rearrange("p (n i t) -> p n t i", t=PACK, i=4),
             )
 
         def keep_awake(count):
@@ -227,30 +227,39 @@ def tile_relationtagger_pa_e_kernel(
 
             return [join, quantise]
 
-        def score_tile(i, first_row):
+        def score_tile(i, first_row, pieces=1):
             b, c = pairs[i]
-            grouped, k_codes, k_planes = tiles_of[(i, "k")]
-            q_grouped, q_codes, q_planes = tiles_of[(i, "q")]
-            acc = psum.tile([P, TOKENS], F32, name="score", bufs=SCORE_BANKS)
-            for s in range(PASSES):
-                if first_row == TOKENS:
-                    n = c * PASSES + s
-                    rows, rows_scale = emb_codes[:, n, :], emb_planes[PLANE_ROWS * n : P, :]
-                else:
-                    rows, rows_scale = q_codes[:, s, first_row : first_row + P], q_planes[:, s, first_row : first_row + P]
-                nc.tensor.matmul_mx(
-                    out=acc[:],
-                    lhsT=rows.bitcast(FP8X4),
-                    lhsT_scale=rows_scale,
-                    rhs=k_codes[:, s, :].bitcast(FP8X4),
-                    rhs_scale=k_planes[:, s, :],
-                    start=(s == 0),
-                    stop=(s == PASSES - 1),
-                )
+            k_codes, k_planes = tiles_of[(i, "k")][1:]
+            q_codes, q_planes = tiles_of[(i, "q")][1:]
+            keys = TOKENS // pieces
+            banks = []
+            for piece in range(pieces):
+                cols = slice(piece * keys, (piece + 1) * keys)
+                acc = psum.tile([P, keys], F32, name="score", bufs=SCORE_BANKS)
+                for s in range(PASSES):
+                    if first_row == TOKENS:
+                        n = c * PASSES + s
+                        rows, rows_scale = emb_codes[:, n, :], emb_planes[PLANE_ROWS * n : P, :]
+                    else:
+                        of_tile = slice(first_row, first_row + P)
+                        rows, rows_scale = q_codes[:, s, of_tile], q_planes[:, s, of_tile]
+                    nc.tensor.matmul_mx(
+                        out=acc[:],
+                        lhsT=rows.bitcast(FP8X4),
+                        lhsT_scale=rows_scale,
+                        rhs=k_codes[:, s, cols].bitcast(FP8X4),
+                        rhs_scale=k_planes[:, s, cols],
+                        start=(s == 0),
+                        stop=(s == PASSES - 1),
+                    )
+                banks.append((cols, acc))
 
             def gate_and_store():
                 gated = work.tile([P, TOKENS], F32, name="gated", bufs=6)
-                nc.vector.tensor_tensor(out=gated[:], in0=acc[:], in1=gate[:, c, b, :], op=mybir.AluOpType.mult)
+                for cols, acc in banks:
+                    nc.vector.tensor_tensor(
+                        out=gated[:, cols], in0=acc[:], in1=gate[:, c, b, cols], op=mybir.AluOpType.mult
+                    )
                 nc.sync.dma_start(out=out[b, c, first_row : first_row + P, :], in_=gated[:])
 
             return [gate_and_store]
@@ -268,12 +277,11 @@ def tile_relationtagger_pa_e_kernel(
         keep_awake(4)
         flip_hidden(0, 0)
         flip_hidden(0, 1)
-        keep_awake(1)
-        spread_first_gate()
+        keep_awake(2)
         sort_planes("k", 0)
         sort_planes("k", 1)
-        quantise_hidden(0, 0)
         sort_words("k", 0, 0, 0)
+        quantise_hidden(0, 0)
         sort_words("k", 0, 0, 1)
         quantise_hidden(0, 1)
 
@@ -295,6 +303,7 @@ def tile_relationtagger_pa_e_kernel(
             (0, 1): [
                 lambda: flip_hidden(0, 2),
                 lambda: flip_hidden(0, 3),
+                spread_first_gate,
                 lambda: sort_words("k", 0, 1, 0),
                 lambda: sort_words("k", 0, 1, 1),
             ],
@@ -325,13 +334,17 @@ def tile_relationtagger_pa_e_kernel(
         for j, row in zip([0, 1, 2, 3, 4], rows_in_turn):
             scores[(last, j)] = [(last - 1, row)]
         scores[(last, 6)] = [(last, label_row)]
-        scores[(last, 7)] = [(last, 0)]
-        scores[(last, 9)] = [(last, P), (last, 2 * P), (last, 3 * P)]
+        scores[(last, 8)] = [(last, 0)]
         for i in range(len(pairs)):
             for j, unit in enumerate(units[i]):
                 step(project(i, *unit))
                 for task in also.get((i, j), []):
                     task()
-                for of_pair, row in scores.get((i, j), []):
-                    step(score_tile(of_pair, row))
-        step([])
+                for tile in scores.get((i, j), []):
+                    step(score_tile(*tile))
+        ends = [score_tile(last, P), score_tile(last, 2 * P)]
+        ends[0][0]()
+        made[-1][0]()
+        ends.append(score_tile(last, 3 * P, 2))
+        ends[1][0]()
+        ends[2][0]()

@@ -41,28 +41,28 @@ def tile_relationtagger_pa_e_kernel(
 
         hidden_sb = keep.tile([P, BATCH, TOKEN_TILES, WIDTH], BF16)
         raw_codes = {
-            "k": keep.tile([P, CHANNELS, PASSES, PASSES, K_PASS], U32, name="wk_raw", align_bytes=64),
-            "q": keep.tile([P, CHANNELS, PASSES, PASSES, K_PASS], U32, name="wq_raw", align_bytes=64),
+            "k": keep.tile([P, CHANNELS, PASSES, PASSES, K_PASS], U32, name="wk_raw", align_bytes=256),
+            "q": keep.tile([P, CHANNELS, PASSES, PASSES, K_PASS], U32, name="wq_raw", align_bytes=256),
         }
         w_codes = {
-            "k": keep.tile([P, CHANNELS * PASSES, WIDTH], U32, name="wk_codes", align_bytes=64),
-            "q": keep.tile([P, CHANNELS * PASSES, WIDTH], U32, name="wq_codes", align_bytes=64),
+            "k": keep.tile([P, CHANNELS * PASSES, WIDTH], U32, name="wk_codes", align_bytes=256),
+            "q": keep.tile([P, CHANNELS * PASSES, WIDTH], U32, name="wq_codes", align_bytes=256),
         }
-        emb_codes = keep.tile([P, CHANNELS * PASSES, LABELS], U32, align_bytes=64)
+        emb_codes = keep.tile([P, CHANNELS * PASSES, LABELS], U32, align_bytes=256)
         raw_planes = {
-            "k": keep.tile([P, WIDTH], U8, name="wk_raw_planes", align_bytes=64),
-            "q": keep.tile([P, WIDTH], U8, name="wq_raw_planes", align_bytes=64),
+            "k": keep.tile([P, WIDTH], U8, name="wk_raw_planes", align_bytes=256),
+            "q": keep.tile([P, WIDTH], U8, name="wq_raw_planes", align_bytes=256),
         }
         w_planes = {
-            "k": keep.tile([P, WIDTH], U8, name="wk_planes", align_bytes=64),
-            "q": keep.tile([P, WIDTH], U8, name="wq_planes", align_bytes=64),
+            "k": keep.tile([P, WIDTH], U8, name="wk_planes", align_bytes=256),
+            "q": keep.tile([P, WIDTH], U8, name="wq_planes", align_bytes=256),
         }
-        emb_planes = keep.tile([P, LABELS], U8, align_bytes=64)
+        emb_planes = keep.tile([P, LABELS], U8, align_bytes=256)
         gate = keep.tile([P, CHANNELS, BATCH, TOKENS], BF16)
         gate_row = keep.tile([P, TOKENS], BF16)
         ones = keep.tile([P, P], BF16)
-        h_codes = keep.tile([P, PASSES, BATCH * TOKENS], U32, align_bytes=64)
-        h_planes = keep.tile([P, PASSES, BATCH * TOKENS], U8, align_bytes=64)
+        h_codes = keep.tile([P, PASSES, BATCH * TOKENS], U32, align_bytes=256)
+        h_planes = keep.tile([P, PASSES, BATCH * TOKENS], U8, align_bytes=256)
         ident_f32 = keep.tile([P, P], F32)
 
         still = keep.tile([P, TOKENS], BF16)
@@ -147,7 +147,7 @@ def tile_relationtagger_pa_e_kernel(
         h_grouped = {}
 
         def flip_hidden(b, u):
-            grouped = work.tile([P, PASSES, P, PACK], BF16, name="h_grouped", bufs=4, align_bytes=64)
+            grouped = work.tile([P, PASSES, P, PACK], BF16, name="h_grouped", bufs=4, align_bytes=256)
             h_grouped[(b, u)] = grouped
             words = hidden_sb[:, b, u, :].bitcast(F32)
             flipped = psum.tile([P, PASSES, 2, P], F32, name="h_flipped", tag="proj", bufs=PROJ_BANKS)
@@ -177,9 +177,9 @@ def tile_relationtagger_pa_e_kernel(
             b, c = pairs[i]
             if (i, which) not in tiles_of:
                 tiles_of[(i, which)] = (
-                    work.tile([P, PASSES, TOKENS, PACK], BF16, name=which + "_grouped", align_bytes=64),
-                    work.tile([P, PASSES, TOKENS], U32, name=which + "_codes", align_bytes=64),
-                    work.tile([P, PASSES, TOKENS], U8, name=which + "_planes", align_bytes=64),
+                    work.tile([P, PASSES, TOKENS, PACK], BF16, name=which + "_grouped", align_bytes=256),
+                    work.tile([P, PASSES, TOKENS], U32, name=which + "_codes", align_bytes=256),
+                    work.tile([P, PASSES, TOKENS], U8, name=which + "_planes", align_bytes=256),
                 )
             grouped, codes, planes = tiles_of[(i, which)]
             tokens = slice(b * TOKENS + first, b * TOKENS + first + count)
@@ -215,7 +215,7 @@ def tile_relationtagger_pa_e_kernel(
                 nc.scalar.copy(out=grouped[:, s, cols, :], in_=bank(0))
                 return [quantise]
 
-            halves = work.tile([P, 2, count, 2], BF16, name="halves", bufs=4, align_bytes=64)
+            halves = work.tile([P, 2, count, 2], BF16, name="halves", bufs=4, align_bytes=256)
             for h in range(2):
                 nc.scalar.copy(out=halves[:, h, :, :], in_=bank(h))
 

@@ -39,14 +39,15 @@ def tile_relationtagger_pa_e_kernel(
         work = ctx.enter_context(tc.tile_pool(name="work", bufs=2))
         psum = ctx.enter_context(tc.psum_pool(name="psum", bufs=1))
 
-        hidden_sb = keep.tile([P, BATCH, TOKEN_TILES, WIDTH], BF16)
+        hidden_sb = keep.tile([P, 1, TOKEN_TILES, WIDTH], BF16)
+        hidden_quads = keep.tile([P, PASSES, TOKENS // 32, P], BF16)
         raw_codes = {
             "k": keep.tile([P, CHANNELS, PASSES, PASSES, K_PASS], U32, name="wk_raw", align_bytes=256),
             "q": keep.tile([P, CHANNELS, PASSES, PASSES, K_PASS], U32, name="wq_raw", align_bytes=256),
         }
         w_codes = {
-            "k": keep.tile([P, CHANNELS * PASSES, WIDTH], U32, name="wk_codes", align_bytes=256),
-            "q": keep.tile([P, CHANNELS * PASSES, WIDTH], U32, name="wq_codes", align_bytes=256),
+            "k": keep.tile([P, CHANNELS, PASSES, PACK, PASSES, P], U32, name="wk_codes", align_bytes=256),
+            "q": keep.tile([P, CHANNELS, PASSES, PACK, PASSES, P], U32, name="wq_codes", align_bytes=256),
         }
         emb_codes = keep.tile([P, CHANNELS * PASSES, LABELS], U32, align_bytes=256)
         raw_planes = {
@@ -54,8 +55,8 @@ def tile_relationtagger_pa_e_kernel(
             "q": keep.tile([P, WIDTH], U8, name="wq_raw_planes", align_bytes=256),
         }
         w_planes = {
-            "k": keep.tile([P, WIDTH], U8, name="wk_planes", align_bytes=256),
-            "q": keep.tile([P, WIDTH], U8, name="wq_planes", align_bytes=256),
+            "k": keep.tile([P, PACK, PASSES, P], U8, name="wk_planes", align_bytes=256),
+            "q": keep.tile([P, PACK, PASSES, P], U8, name="wq_planes", align_bytes=256),
         }
         emb_planes = keep.tile([P, LABELS], U8, align_bytes=256)
         gate = keep.tile([P, CHANNELS, BATCH, TOKENS], BF16)
@@ -111,26 +112,27 @@ def tile_relationtagger_pa_e_kernel(
                 out=emb_codes[:].bitcast(I32),
                 in_=emb_words.rearrange("g p n t -> p g (n t)").bitcast(I32),
             )
-            for u in range(TOKEN_TILES):
-                load_hidden(1, u)
             load_weight("q", Wq_words, 1, 0)
             load_weight("q", Wq_words, 1, 1)
+            for g in range(PASSES):
+                for quad in range(P // 32):
+                    nc.sync.dma_start(
+                        out=hidden_quads[32 * quad : 32 * (quad + 1), g, :, :],
+                        in_=hidden[1].rearrange("(n a) (g q f) -> g q a n f", a=32, g=PASSES, q=4)[g, quad],
+                    )
             for b, c in pairs[1:]:
                 nc.sync.dma_start(out=gate[:, c, b, :], in_=vsum[c, b, :].partition_broadcast(P))
 
-        def sort_planes(which, s):
-            cols = slice(s * K_PASS, (s + 1) * K_PASS)
+        def sort_planes(which):
             nc.vector.tensor_copy(
-                out=w_planes[which][:, cols].rearrange("p (t n i) -> p n t i", t=PACK, i=16),
-                in_=raw_planes[which][:, cols].rearrange("p (n i t) -> p n t i", t=PACK, i=16),
+                out=w_planes[which][:].rearrange("p t s m -> p (t s m)").rearrange("p (t n i) -> p n t i", t=PACK, i=16),
+                in_=raw_planes[which][:].rearrange("p (n i t) -> p n t i", t=PACK, i=16),
             )
 
-        def sort_words(which, c, s, g):
-            n = c * PASSES + g
-            cols = slice(s * K_PASS, (s + 1) * K_PASS)
+        def sort_words(which, c, s, passes=slice(0, PASSES)):
             nc.vector.tensor_copy(
-                out=w_codes[which][:, n, cols].bitcast(I32).rearrange("p (t n i) -> p n t i", t=PACK, i=4),
-                in_=raw_codes[which][:, c, s, g, :].bitcast(I32).rearrange("p (n i t) -> p n t i", t=PACK, i=4),
+                out=w_codes[which][:, c, s, :, passes, :].bitcast(I32).rearrange("p t g (n i) -> p (g n) t i", i=4),
+                in_=raw_codes[which][:, c, s, passes, :].bitcast(I32).rearrange("p g (n i t) -> p (g n) t i", t=PACK, i=4),
             )
 
         def keep_awake(count):
@@ -173,7 +175,39 @@ def tile_relationtagger_pa_e_kernel(
 
         tiles_of = {}
 
-        def project(i, which, first, count, s):
+        turned = {}
+
+        def turn_hidden(turn):
+            chunks = [(g, half) for half in range(2) for g in range(PASSES)]
+            if turn >= 3:
+                g, half = chunks[turn - 3]
+                cols = slice(TOKENS + 2 * P * half, TOKENS + 2 * P * (half + 1))
+                nc.vector.quantize_mx(
+                    out=h_codes[:, g, cols].bitcast(FP8X4),
+                    scales=h_planes[:, g, cols],
+                    in_=turned[(turn - 3, "grouped")][:].rearrange("p r t -> p (r t)"),
+                )
+            if 2 <= turn < 6:
+                joined = work.tile([P, 2 * P, PACK], BF16, name="h_joined", bufs=2, align_bytes=256)
+                turned[(turn - 2, "grouped")] = joined
+                nc.vector.tensor_copy(
+                    out=joined[:].rearrange("p r t -> p (r t)").bitcast(F32).rearrange("p (n a h) -> p n a h", h=2, a=32),
+                    in_=turned[(turn - 2, "flipped")][:].rearrange("p (n h a) -> p n a h", h=2, a=32),
+                )
+            if 1 <= turn < 5:
+                flipped = work.tile([P, 4 * P], F32, name="h_turned", bufs=2, align_bytes=256)
+                turned[(turn - 1, "flipped")] = flipped
+                nc.vector.transpose(out=flipped[:], in_=turned[(turn - 1, "split")][:])
+            if turn < 4:
+                g, half = chunks[turn]
+                split = work.tile([P, 4 * P], F32, name="h_split", bufs=2, align_bytes=256)
+                turned[(turn, "split")] = split
+                nc.scalar.copy(
+                    out=split[:].rearrange("p (n h b) -> p n h b", h=2, b=32),
+                    in_=hidden_quads[:, g, 8 * half : 8 * (half + 1), :].bitcast(F32).rearrange("p n (b h) -> p n h b", h=2),
+                )
+
+        def project(i, which, first, count, s, quantised):
             b, c = pairs[i]
             if (i, which) not in tiles_of:
                 tiles_of[(i, which)] = (
@@ -190,13 +224,12 @@ def tile_relationtagger_pa_e_kernel(
                 acc = psum.tile([P, per_bank, count], F32, name="proj", bufs=PROJ_BANKS)
                 for e in range(per_bank):
                     t = per_bank * h + e
-                    features = slice(s * K_PASS + t * P, s * K_PASS + (t + 1) * P)
                     for g in range(PASSES):
                         n = c * PASSES + g
                         nc.tensor.matmul_mx(
                             out=acc[:, e, :],
-                            lhsT=w_codes[which][:, n, features].bitcast(FP8X4),
-                            lhsT_scale=w_planes[which][PLANE_ROWS * n : P, features],
+                            lhsT=w_codes[which][:, c, s, t, g, :].bitcast(FP8X4),
+                            lhsT_scale=w_planes[which][PLANE_ROWS * n : P, t, s, :],
                             rhs=h_codes[:, g, tokens].bitcast(FP8X4),
                             rhs_scale=h_planes[:, g, tokens],
                             start=(g == 0),
@@ -204,16 +237,18 @@ def tile_relationtagger_pa_e_kernel(
                         )
                 return acc[:].rearrange("p e r -> p r e")
 
+            ready = slice(first + count - quantised, first + count)
+
             def quantise():
                 nc.vector.quantize_mx(
-                    out=codes[:, s, cols].bitcast(FP8X4),
-                    scales=planes[:, s, cols],
-                    in_=grouped[:, s, cols, :].rearrange("p r t -> p (r t)"),
+                    out=codes[:, s, ready].bitcast(FP8X4),
+                    scales=planes[:, s, ready],
+                    in_=grouped[:, s, ready, :].rearrange("p r t -> p (r t)"),
                 )
 
             if per_bank == PACK:
                 nc.scalar.copy(out=grouped[:, s, cols, :], in_=bank(0))
-                return [quantise]
+                return [quantise] if quantised else []
 
             halves = work.tile([P, 2, count, 2], BF16, name="halves", bufs=4, align_bytes=256)
             for h in range(2):
@@ -265,6 +300,7 @@ def tile_relationtagger_pa_e_kernel(
             return [gate_and_store]
 
         pairs = [(b, c) for b in range(BATCH) for c in range(CHANNELS)]
+        last = len(pairs) - 1
         made = []
 
         def step(tasks):
@@ -273,75 +309,97 @@ def tile_relationtagger_pa_e_kernel(
                 if len(made) > lag and len(made[-1 - lag]) >= lag:
                     made[-1 - lag][lag - 1]()
 
+        def unit(i, which, first, count, s, quantised=None):
+            step(project(i, which, first, count, s, count if quantised is None else quantised))
+
+        def score(i, first_row):
+            step(score_tile(i, first_row))
+
         load_all()
         keep_awake(4)
         flip_hidden(0, 0)
         flip_hidden(0, 1)
         keep_awake(2)
-        sort_planes("k", 0)
-        sort_planes("k", 1)
-        sort_words("k", 0, 0, 0)
+        sort_planes("k")
+        sort_words("k", 0, 0, slice(0, 1))
         quantise_hidden(0, 0)
-        sort_words("k", 0, 0, 1)
+        sort_words("k", 0, 0, slice(1, 2))
         quantise_hidden(0, 1)
 
         label_row = TOKENS
-        wide = [(0, 2 * P), (2 * P, 2 * P)]
-        mixed = [(0, 2 * P), (2 * P, P), (3 * P, P)]
-
-        def units_of(which, pieces):
-            return [(which, first, count, s) for first, count in pieces for s in range(PASSES)]
-
-        first_keys = [("k", 0, P, 0), ("k", P, P, 0), ("k", 0, 2 * P, 1)] + units_of("k", wide[1:])
-        units = [
-            first_keys + units_of("q", wide),
-            units_of("k", wide) + units_of("q", wide),
-            units_of("k", wide) + units_of("q", wide),
-            units_of("k", wide) + units_of("q", mixed),
-        ]
-        also = {
-            (0, 1): [
-                lambda: flip_hidden(0, 2),
-                lambda: flip_hidden(0, 3),
-                spread_first_gate,
-                lambda: sort_words("k", 0, 1, 0),
-                lambda: sort_words("k", 0, 1, 1),
-            ],
-            (0, 2): [
-                lambda: quantise_hidden(0, 2),
-                lambda: quantise_hidden(0, 3),
-                lambda: sort_planes("q", 0),
-                lambda: sort_planes("q", 1),
-                lambda: sort_words("q", 0, 0, 0),
-                lambda: sort_words("q", 0, 0, 1),
-            ],
-            (0, 3): [lambda: sort_words("q", 0, 1, 0), lambda: sort_words("q", 0, 1, 1)],
-            (0, 5): [lambda: sort_words("k", 1, 0, 0), lambda: sort_words("k", 1, 0, 1)],
-            (0, 6): [lambda: sort_words("k", 1, 1, 0), lambda: sort_words("k", 1, 1, 1)],
-            (1, 0): [lambda: sort_words("q", 1, 0, 0), lambda: sort_words("q", 1, 0, 1)],
-            (1, 2): [lambda: sort_words("q", 1, 1, 0), lambda: sort_words("q", 1, 1, 1)],
-            (1, 3): [lambda: flip_hidden(1, 0), lambda: flip_hidden(1, 1)],
-            (1, 4): [lambda: quantise_hidden(1, 0), lambda: quantise_hidden(1, 1)],
-            (1, 5): [lambda: flip_hidden(1, 2), lambda: flip_hidden(1, 3)],
-            (1, 6): [lambda: quantise_hidden(1, 2), lambda: quantise_hidden(1, 3)],
-        }
-        rows_in_turn = [label_row, 0, P, 2 * P, 3 * P]
-        last = len(pairs) - 1
-        scores = {}
-        for i in range(1, last):
-            for j, row in zip([1, 2, 4, 5, 7], rows_in_turn):
-                scores[(i, j)] = [(i - 1, row)]
-        for j, row in zip([0, 1, 2, 3, 4], rows_in_turn):
-            scores[(last, j)] = [(last - 1, row)]
-        scores[(last, 6)] = [(last, label_row)]
-        scores[(last, 8)] = [(last, 0)]
-        for i in range(len(pairs)):
-            for j, unit in enumerate(units[i]):
-                step(project(i, *unit))
-                for task in also.get((i, j), []):
-                    task()
-                for tile in scores.get((i, j), []):
-                    step(score_tile(*tile))
+        unit(0, "k", 0, P, 0)
+        unit(0, "k", P, P, 0)
+        flip_hidden(0, 2)
+        flip_hidden(0, 3)
+        spread_first_gate()
+        sort_words("k", 0, 1, slice(0, 1))
+        sort_words("k", 0, 1, slice(1, 2))
+        unit(0, "k", 0, 2 * P, 1)
+        quantise_hidden(0, 2)
+        quantise_hidden(0, 3)
+        sort_planes("q")
+        sort_words("q", 0, 0)
+        unit(0, "k", 2 * P, 2 * P, 0)
+        sort_words("q", 0, 1)
+        unit(0, "k", 2 * P, 2 * P, 1)
+        unit(0, "q", 0, 2 * P, 0)
+        sort_words("k", 1, 0)
+        unit(0, "q", 0, 2 * P, 1)
+        sort_words("k", 1, 1)
+        unit(0, "q", 2 * P, 2 * P, 0)
+        unit(0, "q", 2 * P, 2 * P, 1)
+        unit(1, "k", 0, 2 * P, 0)
+        sort_words("q", 1, 0)
+        score(0, label_row)
+        unit(1, "k", 0, 2 * P, 1)
+        score(0, 0)
+        unit(1, "k", 2 * P, 2 * P, 0)
+        sort_words("q", 1, 1)
+        turn_hidden(0)
+        turn_hidden(1)
+        score(0, P)
+        unit(1, "k", 2 * P, 2 * P, 1)
+        turn_hidden(2)
+        unit(1, "q", 0, 2 * P, 0)
+        turn_hidden(3)
+        turn_hidden(4)
+        unit(1, "q", 0, 2 * P, 1)
+        turn_hidden(5)
+        turn_hidden(6)
+        score(0, 2 * P)
+        unit(1, "q", 2 * P, 2 * P, 0)
+        score(0, 3 * P)
+        unit(1, "q", 2 * P, 2 * P, 1)
+        unit(2, "k", 0, 2 * P, 0)
+        unit(2, "k", 0, 2 * P, 1)
+        score(1, label_row)
+        unit(2, "k", 2 * P, 2 * P, 0)
+        score(1, 0)
+        unit(2, "k", 2 * P, 2 * P, 1)
+        unit(2, "q", 0, 2 * P, 0)
+        score(1, P)
+        unit(2, "q", 0, 2 * P, 1)
+        score(1, 2 * P)
+        unit(2, "q", 2 * P, 2 * P, 0)
+        unit(2, "q", 2 * P, 2 * P, 1)
+        score(1, 3 * P)
+        unit(3, "k", 0, 2 * P, 0)
+        score(2, label_row)
+        unit(3, "k", 0, 2 * P, 1)
+        score(2, 0)
+        unit(3, "k", 2 * P, 2 * P, 0)
+        score(2, P)
+        unit(3, "k", 2 * P, 2 * P, 1)
+        score(2, 2 * P)
+        unit(3, "q", 0, 2 * P, 0)
+        score(2, 3 * P)
+        unit(3, "q", 0, 2 * P, 1)
+        unit(3, "q", 2 * P, P, 0)
+        score(3, label_row)
+        unit(3, "q", 2 * P, P, 1)
+        unit(3, "q", 3 * P, P, 0)
+        score(3, 0)
+        unit(3, "q", 3 * P, P, 1)
         ends = [score_tile(last, P), score_tile(last, 2 * P)]
         ends[0][0]()
         made[-1][0]()

@@ -40,7 +40,7 @@ def tile_relationtagger_pa_e_kernel(
         psum = ctx.enter_context(tc.psum_pool(name="psum", bufs=1))
 
         hidden_sb = keep.tile([P, 1, TOKEN_TILES, WIDTH], BF16)
-        hidden_quads = keep.tile([P, PASSES, TOKENS // 32, P], BF16)
+        hidden_quads = keep.tile([P, 2, PASSES, 8, P], BF16)
         raw_codes = {
             "k": keep.tile([P, CHANNELS, PASSES, PASSES, K_PASS], U32, name="wk_raw", align_bytes=256),
             "q": keep.tile([P, CHANNELS, PASSES, PASSES, K_PASS], U32, name="wq_raw", align_bytes=256),
@@ -60,16 +60,12 @@ def tile_relationtagger_pa_e_kernel(
         }
         emb_planes = keep.tile([P, LABELS], U8, align_bytes=256)
         gate = keep.tile([P, CHANNELS, BATCH, TOKENS], BF16)
-        gate_row = keep.tile([P, TOKENS], BF16)
-        ones = keep.tile([P, P], BF16)
         h_codes = keep.tile([P, PASSES, BATCH * TOKENS], U32, align_bytes=256)
         h_planes = keep.tile([P, PASSES, BATCH * TOKENS], U8, align_bytes=256)
         ident_f32 = keep.tile([P, P], F32)
 
         still = keep.tile([P, TOKENS], BF16)
         nc.gpsimd.memset(still[:].bitcast(F32), 0.0)
-        nc.gpsimd.memset(gate_row[:].bitcast(F32), 0.0)
-        nc.gpsimd.memset(ones[:], 1.0)
         make_identity(nc, ident_f32[:])
         for planes in (raw_planes["k"], raw_planes["q"], emb_planes):
             nc.vector.memset(planes[:].bitcast(I32), 0)
@@ -93,12 +89,23 @@ def tile_relationtagger_pa_e_kernel(
                     in_=words[c * PASSES + g].rearrange("p n t -> p (n t)").bitcast(I32)[:, cols],
                 )
 
+        def load_gate(b, c):
+            nc.sync.dma_start(out=gate[:, c, b, :], in_=vsum[c, b, :].partition_broadcast(P))
+
+        def load_quads(half):
+            tokens = hidden[1, 256 * half : 256 * (half + 1), :]
+            for g in range(PASSES):
+                for quad in (0, 2, 1, 3):
+                    nc.sync.dma_start(
+                        out=hidden_quads[32 * quad : 32 * (quad + 1), half, g, :, :],
+                        in_=tokens.rearrange("(n a) (g q f) -> g q a n f", a=32, g=PASSES, q=4)[g, quad],
+                    )
+
         def load_all():
             load_hidden(0, 0)
             load_planes(raw_planes["k"], Wk_scales)
             load_hidden(0, 1)
             load_weight("k", Wk_words, 0, 0)
-            nc.sync.dma_start(out=gate_row[0:1], in_=vsum[0, 0:1, :])
             load_hidden(0, 2)
             load_hidden(0, 3)
             load_weight("k", Wk_words, 0, 1)
@@ -107,21 +114,18 @@ def tile_relationtagger_pa_e_kernel(
             load_weight("q", Wq_words, 0, 1)
             load_weight("k", Wk_words, 1, 0)
             load_weight("k", Wk_words, 1, 1)
+            load_gate(*pairs[0])
             load_planes(emb_planes, emb_scales)
             nc.sync.dma_start(
                 out=emb_codes[:].bitcast(I32),
                 in_=emb_words.rearrange("g p n t -> p g (n t)").bitcast(I32),
             )
             load_weight("q", Wq_words, 1, 0)
+            load_quads(0)
             load_weight("q", Wq_words, 1, 1)
-            for g in range(PASSES):
-                for quad in range(P // 32):
-                    nc.sync.dma_start(
-                        out=hidden_quads[32 * quad : 32 * (quad + 1), g, :, :],
-                        in_=hidden[1].rearrange("(n a) (g q f) -> g q a n f", a=32, g=PASSES, q=4)[g, quad],
-                    )
-            for b, c in pairs[1:]:
-                nc.sync.dma_start(out=gate[:, c, b, :], in_=vsum[c, b, :].partition_broadcast(P))
+            load_quads(1)
+            for pair in pairs[1:]:
+                load_gate(*pair)
 
         def sort_planes(which):
             nc.vector.tensor_copy(
@@ -139,12 +143,6 @@ def tile_relationtagger_pa_e_kernel(
             for turn in range(count):
                 idle = psum.tile([P, TOKENS], F32, name="idle", tag="score", bufs=SCORE_BANKS)
                 nc.tensor.matmul(out=idle[:], lhsT=still[:, :P], rhs=still[:], start=True, stop=True)
-
-        def spread_first_gate():
-            b, c = pairs[0]
-            spread = psum.tile([P, TOKENS], F32, name="spread", tag="score", bufs=SCORE_BANKS)
-            nc.tensor.matmul(out=spread[:], lhsT=ones[:], rhs=gate_row[:], start=True, stop=True)
-            nc.scalar.copy(out=gate[:, c, b, :], in_=spread[:])
 
         h_grouped = {}
 
@@ -204,7 +202,7 @@ def tile_relationtagger_pa_e_kernel(
                 turned[(turn, "split")] = split
                 nc.scalar.copy(
                     out=split[:].rearrange("p (n h b) -> p n h b", h=2, b=32),
-                    in_=hidden_quads[:, g, 8 * half : 8 * (half + 1), :].bitcast(F32).rearrange("p n (b h) -> p n h b", h=2),
+                    in_=hidden_quads[:, half, g, :, :].bitcast(F32).rearrange("p n (b h) -> p n h b", h=2),
                 )
 
         def project(i, which, first, count, s, quantised):
@@ -295,7 +293,7 @@ def tile_relationtagger_pa_e_kernel(
                     nc.vector.tensor_tensor(
                         out=gated[:, cols], in0=acc[:], in1=gate[:, c, b, cols], op=mybir.AluOpType.mult
                     )
-                nc.sync.dma_start(out=out[b, c, first_row : first_row + P, :], in_=gated[:])
+                    nc.sync.dma_start(out=out[b, c, first_row : first_row + P, cols], in_=gated[:, cols])
 
             return [gate_and_store]
 
@@ -331,7 +329,6 @@ def tile_relationtagger_pa_e_kernel(
         unit(0, "k", P, P, 0)
         flip_hidden(0, 2)
         flip_hidden(0, 3)
-        spread_first_gate()
         sort_words("k", 0, 1, slice(0, 1))
         sort_words("k", 0, 1, slice(1, 2))
         unit(0, "k", 0, 2 * P, 1)

@@ -316,8 +316,9 @@ def tile_relationtagger_pa_e_kernel(
         load_all()
         keep_awake(4)
         flip_hidden(0, 0)
+        keep_awake(1)
         flip_hidden(0, 1)
-        keep_awake(2)
+        keep_awake(3)
         sort_planes("k")
         sort_words("k", 0, 0, slice(0, 1))
         quantise_hidden(0, 0)

@@ -218,22 +218,23 @@ def tile_relationtagger_pa_e_kernel(
             cols = slice(first, first + count)
             per_bank = TOKENS // count
 
-            def bank(h):
-                acc = psum.tile([P, per_bank, count], F32, name="proj", bufs=PROJ_BANKS)
-                for e in range(per_bank):
-                    t = per_bank * h + e
-                    for g in range(PASSES):
-                        n = c * PASSES + g
-                        nc.tensor.matmul_mx(
-                            out=acc[:, e, :],
-                            lhsT=w_codes[which][:, c, s, t, g, :].bitcast(FP8X4),
-                            lhsT_scale=w_planes[which][PLANE_ROWS * n : P, t, s, :],
-                            rhs=h_codes[:, g, tokens].bitcast(FP8X4),
-                            rhs_scale=h_planes[:, g, tokens],
-                            start=(g == 0),
-                            stop=(g == PASSES - 1),
-                        )
-                return acc[:].rearrange("p e r -> p r e")
+            def banks(total):
+                accs = [psum.tile([P, per_bank, count], F32, name="proj", bufs=PROJ_BANKS) for h in range(total)]
+                order = [(t, g) for t in range(PACK) for g in range(PASSES)]
+                if total == 2:
+                    order = [(0, 0), (2, 0), (0, 1), (1, 0), (2, 1), (1, 1), (3, 0), (3, 1)]
+                for t, g in order:
+                    n = c * PASSES + g
+                    nc.tensor.matmul_mx(
+                        out=accs[t // per_bank][:, t % per_bank, :],
+                        lhsT=w_codes[which][:, c, s, t, g, :].bitcast(FP8X4),
+                        lhsT_scale=w_planes[which][PLANE_ROWS * n : P, t, s, :],
+                        rhs=h_codes[:, g, tokens].bitcast(FP8X4),
+                        rhs_scale=h_planes[:, g, tokens],
+                        start=(g == 0),
+                        stop=(g == PASSES - 1),
+                    )
+                return [acc[:].rearrange("p e r -> p r e") for acc in accs]
 
             ready = slice(first + count - quantised, first + count)
 
@@ -245,12 +246,12 @@ def tile_relationtagger_pa_e_kernel(
                 )
 
             if per_bank == PACK:
-                nc.scalar.copy(out=grouped[:, s, cols, :], in_=bank(0))
+                nc.scalar.copy(out=grouped[:, s, cols, :], in_=banks(1)[0])
                 return [quantise] if quantised else []
 
             halves = work.tile([P, 2, count, 2], BF16, name="halves", bufs=4, align_bytes=256)
-            for h in range(2):
-                nc.scalar.copy(out=halves[:, h, :, :], in_=bank(h))
+            for h, full in enumerate(banks(2)):
+                nc.scalar.copy(out=halves[:, h, :, :], in_=full)
 
             def join():
                 nc.vector.tensor_copy(

from contextlib import ExitStack

import concourse.mybir as mybir
from concourse.masks import make_identity

F32 = mybir.dt.float32
BF16 = mybir.dt.bfloat16
I32 = mybir.dt.int32
U32 = mybir.dt.uint32
U8 = mybir.dt.uint8
FP8X4 = mybir.dt.float8_e4m3fn_x4

CHANNELS = 2
BATCH = 2
TOKENS = 512
WIDTH = 1024
LABELS = 128

P = 128
PACK = 4
K_PASS = P * PACK
PASSES = WIDTH // K_PASS
TOKEN_TILES = TOKENS // P
PLANE_ROWS = 4

PROJ_BANKS = 5
SCORE_BANKS = 3

FLOPS = 2 * BATCH * CHANNELS * (2 * TOKENS * WIDTH * WIDTH + (TOKENS + LABELS) * WIDTH * TOKENS)


def tile_relationtagger_pa_e_kernel(
    tc, hidden, emb_words, emb_scales, Wk_words, Wk_scales, Wq_words, Wq_scales, vsum, out
):
    nc = tc.nc
    with ExitStack() as ctx:
        ctx.enter_context(tc.manual_schedule())
        keep = ctx.enter_context(tc.tile_pool(name="keep", bufs=1))
        work = ctx.enter_context(tc.tile_pool(name="work", bufs=2))
        psum = ctx.enter_context(tc.psum_pool(name="psum", bufs=1))

        hidden_sb = keep.tile([P, 1, TOKEN_TILES, WIDTH], BF16)
        hidden_quads = keep.tile([P, 2, PASSES, 8, P], BF16)
        raw_codes = {
            "k": keep.tile([P, CHANNELS, PASSES, PASSES, K_PASS], U32, name="wk_raw", align_bytes=256),
            "q": keep.tile([P, CHANNELS, PASSES, PASSES, K_PASS], U32, name="wq_raw", align_bytes=256),
        }
        w_codes = {
            "k": keep.tile([P, CHANNELS, PASSES, PACK, PASSES, P], U32, name="wk_codes", align_bytes=256),
            "q": keep.tile([P, CHANNELS, PASSES, PACK, PASSES, P], U32, name="wq_codes", align_bytes=256),
        }
        emb_codes = keep.tile([P, CHANNELS * PASSES, LABELS], U32, align_bytes=256)
        raw_planes = {
            "k": keep.tile([P, WIDTH], U8, name="wk_raw_planes", align_bytes=256),
            "q": keep.tile([P, WIDTH], U8, name="wq_raw_planes", align_bytes=256),
        }
        w_planes = {
            "k": keep.tile([P, PACK, PASSES, P], U8, name="wk_planes", align_bytes=256),
            "q": keep.tile([P, PACK, PASSES, P], U8, name="wq_planes", align_bytes=256),
        }
        emb_planes = keep.tile([P, LABELS], U8, align_bytes=256)
        gate = keep.tile([P, CHANNELS, BATCH, TOKENS], BF16)
        h_codes = keep.tile([P, PASSES, BATCH * TOKENS], U32, align_bytes=256)
        h_planes = keep.tile([P, PASSES, BATCH * TOKENS], U8, align_bytes=256)
        ident_f32 = keep.tile([P, P], F32)

        still = keep.tile([P, TOKENS], BF16)
        nc.gpsimd.memset(still[:].bitcast(F32), 0.0)
        make_identity(nc, ident_f32[:])
        for planes in (raw_planes["k"], raw_planes["q"], emb_planes):
            nc.vector.memset(planes[:].bitcast(I32), 0)

        def load_planes(planes, scales):
            for quad in range(P // 32):
                rows = slice(PLANE_ROWS * quad, PLANE_ROWS * (quad + 1))
                nc.sync.dma_start(
                    out=planes[32 * quad : 32 * quad + 16, :].bitcast(I32),
                    in_=scales[:, rows, :].bitcast(I32),
                )

        def load_hidden(b, u):
            nc.sync.dma_start(out=hidden_sb[:, b, u, :], in_=hidden[b, u * P : (u + 1) * P, :])

        def load_weight(which, words, c, s):
            cols = slice(s * K_PASS, (s + 1) * K_PASS)
            for g in range(PASSES):
                nc.sync.dma_start(
                    out=raw_codes[which][:, c, s, g, :].bitcast(I32),
                    in_=words[c * PASSES + g].rearrange("p n t -> p (n t)").bitcast(I32)[:, cols],
                )

        def load_gate(b, c):
            nc.sync.dma_start(out=gate[:, c, b, :], in_=vsum[c, b, :].partition_broadcast(P))

        def load_quads(half):
            tokens = hidden[1, 256 * half : 256 * (half + 1), :]
            for g in range(PASSES):
                for quad in (0, 2, 1, 3):
                    nc.sync.dma_start(
                        out=hidden_quads[32 * quad : 32 * (quad + 1), half, g, :, :],
                        in_=tokens.rearrange("(n a) (g q f) -> g q a n f", a=32, g=PASSES, q=4)[g, quad],
                    )

        def load_all():
            load_hidden(0, 0)
            load_planes(raw_planes["k"], Wk_scales)
            load_hidden(0, 1)
            load_weight("k", Wk_words, 0, 0)
            load_hidden(0, 2)
            load_hidden(0, 3)
            load_weight("k", Wk_words, 0, 1)
            load_planes(raw_planes["q"], Wq_scales)
            load_weight("q", Wq_words, 0, 0)
            load_weight("q", Wq_words, 0, 1)
            load_weight("k", Wk_words, 1, 0)
            load_weight("k", Wk_words, 1, 1)
            load_gate(*pairs[0])
            load_planes(emb_planes, emb_scales)
            nc.sync.dma_start(
                out=emb_codes[:].bitcast(I32),
                in_=emb_words.rearrange("g p n t -> p g (n t)").bitcast(I32),
            )
            load_weight("q", Wq_words, 1, 0)
            load_quads(0)
            load_weight("q", Wq_words, 1, 1)
            load_quads(1)
            for pair in pairs[1:]:
                load_gate(*pair)

        def sort_planes(which):
            nc.vector.tensor_copy(
                out=w_planes[which][:].rearrange("p t s m -> p (t s m)").rearrange("p (t n i) -> p n t i", t=PACK, i=16),
                in_=raw_planes[which][:].rearrange("p (n i t) -> p n t i", t=PACK, i=16),
            )

        def sort_words(which, c, s, passes=slice(0, PASSES)):
            nc.vector.tensor_copy(
                out=w_codes[which][:, c, s, :, passes, :].bitcast(I32).rearrange("p t g (n i) -> p (g n) t i", i=4),
                in_=raw_codes[which][:, c, s, passes, :].bitcast(I32).rearrange("p g (n i t) -> p (g n) t i", t=PACK, i=4),
            )

        def keep_awake(count):
            for turn in range(count):
                idle = psum.tile([P, TOKENS], F32, name="idle", tag="score", bufs=SCORE_BANKS)
                nc.tensor.matmul(out=idle[:], lhsT=still[:, :P], rhs=still[:], start=True, stop=True)

        h_grouped = {}

        def flip_hidden(b, u):
            grouped = work.tile([P, PASSES, P, PACK], BF16, name="h_grouped", bufs=4, align_bytes=256)
            h_grouped[(b, u)] = grouped
            words = hidden_sb[:, b, u, :].bitcast(F32)
            flipped = psum.tile([P, PASSES, 2, P], F32, name="h_flipped", tag="proj", bufs=PROJ_BANKS)
            for g in range(PASSES):
                for h in range(2):
                    first = (K_PASS // 2) * g + h
                    nc.tensor.transpose(
                        flipped[:, g, h, :], words[:, first : (K_PASS // 2) * (g + 1) : 2], ident_f32[:]
                    )
            nc.scalar.copy(
                out=grouped[:].bitcast(F32),
                in_=flipped[:].rearrange("p g h r -> p g r h"),
            )

        def quantise_hidden(b, u):
            for g in range(PASSES):
                cols = slice(b * TOKENS + u * P, b * TOKENS + (u + 1) * P)
                nc.vector.quantize_mx(
                    out=h_codes[:, g, cols].bitcast(FP8X4),
                    scales=h_planes[:, g, cols],
                    in_=h_grouped[(b, u)][:, g, :, :].rearrange("p s t -> p (s t)"),
                )

        tiles_of = {}

        turned = {}

        def turn_hidden(turn):
            chunks = [(g, half) for half in range(2) for g in range(PASSES)]
            if turn >= 3:
                g, half = chunks[turn - 3]
                cols = slice(TOKENS + 2 * P * half, TOKENS + 2 * P * (half + 1))
                nc.vector.quantize_mx(
                    out=h_codes[:, g, cols].bitcast(FP8X4),
                    scales=h_planes[:, g, cols],
                    in_=turned[(turn - 3, "grouped")][:].rearrange("p r t -> p (r t)"),
                )
            if 2 <= turn < 6:
                joined = work.tile([P, 2 * P, PACK], BF16, name="h_joined", bufs=2, align_bytes=256)
                turned[(turn - 2, "grouped")] = joined
                nc.vector.tensor_copy(
                    out=joined[:].rearrange("p r t -> p (r t)").bitcast(F32).rearrange("p (n a h) -> p n a h", h=2, a=32),
                    in_=turned[(turn - 2, "flipped")][:].rearrange("p (n h a) -> p n a h", h=2, a=32),
                )
            if 1 <= turn < 5:
                flipped = work.tile([P, 4 * P], F32, name="h_turned", bufs=2, align_bytes=256)
                turned[(turn - 1, "flipped")] = flipped
                nc.vector.transpose(out=flipped[:], in_=turned[(turn - 1, "split")][:])
            if turn < 4:
                g, half = chunks[turn]
                split = work.tile([P, 4 * P], F32, name="h_split", bufs=2, align_bytes=256)
                turned[(turn, "split")] = split
                nc.scalar.copy(
                    out=split[:].rearrange("p (n h b) -> p n h b", h=2, b=32),
                    in_=hidden_quads[:, half, g, :, :].bitcast(F32).rearrange("p n (b h) -> p n h b", h=2),
                )

        def project(i, which, first, count, s, quantised):
            b, c = pairs[i]
            if (i, which) not in tiles_of:
                tiles_of[(i, which)] = (
                    work.tile([P, PASSES, TOKENS, PACK], BF16, name=which + "_grouped", align_bytes=256),
                    work.tile([P, PASSES, TOKENS], U32, name=which + "_codes", align_bytes=256),
                    work.tile([P, PASSES, TOKENS], U8, name=which + "_planes", align_bytes=256),
                )
            grouped, codes, planes = tiles_of[(i, which)]
            tokens = slice(b * TOKENS + first, b * TOKENS + first + count)
            cols = slice(first, first + count)
            per_bank = TOKENS // count

            def banks(total):
                accs = [psum.tile([P, per_bank, count], F32, name="proj", bufs=PROJ_BANKS) for h in range(total)]
                order = [(t, g) for t in range(PACK) for g in range(PASSES)]
                if total == 2:
                    order = [(0, 0), (2, 0), (0, 1), (1, 0), (2, 1), (1, 1), (3, 0), (3, 1)]
                for t, g in order:
                    n = c * PASSES + g
                    nc.tensor.matmul_mx(
                        out=accs[t // per_bank][:, t % per_bank, :],
                        lhsT=w_codes[which][:, c, s, t, g, :].bitcast(FP8X4),
                        lhsT_scale=w_planes[which][PLANE_ROWS * n : P, t, s, :],
                        rhs=h_codes[:, g, tokens].bitcast(FP8X4),
                        rhs_scale=h_planes[:, g, tokens],
                        start=(g == 0),
                        stop=(g == PASSES - 1),
                    )
                return [acc[:].rearrange("p e r -> p r e") for acc in accs]

            ready = slice(first + count - quantised, first + count)

            def quantise():
                nc.vector.quantize_mx(
                    out=codes[:, s, ready].bitcast(FP8X4),
                    scales=planes[:, s, ready],
                    in_=grouped[:, s, ready, :].rearrange("p r t -> p (r t)"),
                )

            if per_bank == PACK:
                nc.scalar.copy(out=grouped[:, s, cols, :], in_=banks(1)[0])
                return [quantise] if quantised else []

            halves = work.tile([P, 2, count, 2], BF16, name="halves", bufs=4, align_bytes=256)
            for h, full in enumerate(banks(2)):
                nc.scalar.copy(out=halves[:, h, :, :], in_=full)

            def join():
                nc.vector.tensor_copy(
                    out=grouped[:, s, cols, :].rearrange("p r t -> p (r t)").bitcast(F32).rearrange("p (r h) -> p r h", h=2),
                    in_=halves[:].rearrange("p h r e -> p (h r e)").bitcast(F32).rearrange("p (h r) -> p r h", h=2),
                )

            return [join, quantise]

        def score_tile(i, first_row, pieces=1):
            b, c = pairs[i]
            k_codes, k_planes = tiles_of[(i, "k")][1:]
            q_codes, q_planes = tiles_of[(i, "q")][1:]
            keys = TOKENS // pieces
            banks = []
            for piece in range(pieces):
                cols = slice(piece * keys, (piece + 1) * keys)
                acc = psum.tile([P, keys], F32, name="score", bufs=SCORE_BANKS)
                for s in range(PASSES):
                    if first_row == TOKENS:
                        n = c * PASSES + s
                        rows, rows_scale = emb_codes[:, n, :], emb_planes[PLANE_ROWS * n : P, :]
                    else:
                        of_tile = slice(first_row, first_row + P)
                        rows, rows_scale = q_codes[:, s, of_tile], q_planes[:, s, of_tile]
                    nc.tensor.matmul_mx(
                        out=acc[:],
                        lhsT=rows.bitcast(FP8X4),
                        lhsT_scale=rows_scale,
                        rhs=k_codes[:, s, cols].bitcast(FP8X4),
                        rhs_scale=k_planes[:, s, cols],
                        start=(s == 0),
                        stop=(s == PASSES - 1),
                    )
                banks.append((cols, acc))

            def gate_and_store():
                gated = work.tile([P, TOKENS], F32, name="gated", bufs=6)
                for cols, acc in banks:
                    nc.vector.tensor_tensor(
                        out=gated[:, cols], in0=acc[:], in1=gate[:, c, b, cols], op=mybir.AluOpType.mult
                    )
                    nc.sync.dma_start(out=out[b, c, first_row : first_row + P, cols], in_=gated[:, cols])

            return [gate_and_store]

        pairs = [(b, c) for b in range(BATCH) for c in range(CHANNELS)]
        last = len(pairs) - 1
        made = []

        def step(tasks):
            made.append(tasks)
            for lag in (1, 2):
                if len(made) > lag and len(made[-1 - lag]) >= lag:
                    made[-1 - lag][lag - 1]()

        def unit(i, which, first, count, s, quantised=None):
            step(project(i, which, first, count, s, count if quantised is None else quantised))

        def score(i, first_row):
            step(score_tile(i, first_row))

        load_all()
        keep_awake(4)
        flip_hidden(0, 0)
        keep_awake(1)
        flip_hidden(0, 1)
        keep_awake(3)
        sort_planes("k")
        sort_words("k", 0, 0, slice(0, 1))
        quantise_hidden(0, 0)
        sort_words("k", 0, 0, slice(1, 2))
        quantise_hidden(0, 1)

        label_row = TOKENS
        unit(0, "k", 0, P, 0)
        unit(0, "k", P, P, 0)
        flip_hidden(0, 2)
        flip_hidden(0, 3)
        sort_words("k", 0, 1, slice(0, 1))
        sort_words("k", 0, 1, slice(1, 2))
        unit(0, "k", 0, 2 * P, 1)
        quantise_hidden(0, 2)
        quantise_hidden(0, 3)
        sort_planes("q")
        sort_words("q", 0, 0)
        unit(0, "k", 2 * P, 2 * P, 0)
        sort_words("q", 0, 1)
        unit(0, "k", 2 * P, 2 * P, 1)
        unit(0, "q", 0, 2 * P, 0)
        sort_words("k", 1, 0)
        unit(0, "q", 0, 2 * P, 1)
        sort_words("k", 1, 1)
        unit(0, "q", 2 * P, 2 * P, 0)
        unit(0, "q", 2 * P, 2 * P, 1)
        unit(1, "k", 0, 2 * P, 0)
        sort_words("q", 1, 0)
        score(0, label_row)
        unit(1, "k", 0, 2 * P, 1)
        score(0, 0)
        unit(1, "k", 2 * P, 2 * P, 0)
        sort_words("q", 1, 1)
        turn_hidden(0)
        turn_hidden(1)
        score(0, P)
        unit(1, "k", 2 * P, 2 * P, 1)
        turn_hidden(2)
        unit(1, "q", 0, 2 * P, 0)
        turn_hidden(3)
        turn_hidden(4)
        unit(1, "q", 0, 2 * P, 1)
        turn_hidden(5)
        turn_hidden(6)
        score(0, 2 * P)
        unit(1, "q", 2 * P, 2 * P, 0)
        score(0, 3 * P)
        unit(1, "q", 2 * P, 2 * P, 1)
        unit(2, "k", 0, 2 * P, 0)
        unit(2, "k", 0, 2 * P, 1)
        score(1, label_row)
        unit(2, "k", 2 * P, 2 * P, 0)
        score(1, 0)
        unit(2, "k", 2 * P, 2 * P, 1)
        unit(2, "q", 0, 2 * P, 0)
        score(1, P)
        unit(2, "q", 0, 2 * P, 1)
        score(1, 2 * P)
        unit(2, "q", 2 * P, 2 * P, 0)
        unit(2, "q", 2 * P, 2 * P, 1)
        score(1, 3 * P)
        unit(3, "k", 0, 2 * P, 0)
        score(2, label_row)
        unit(3, "k", 0, 2 * P, 1)
        score(2, 0)
        unit(3, "k", 2 * P, 2 * P, 0)
        score(2, P)
        unit(3, "k", 2 * P, 2 * P, 1)
        score(2, 2 * P)
        unit(3, "q", 0, 2 * P, 0)
        score(2, 3 * P)
        unit(3, "q", 0, 2 * P, 1)
        unit(3, "q", 2 * P, P, 0)
        score(3, label_row)
        unit(3, "q", 2 * P, P, 1)
        unit(3, "q", 3 * P, P, 0)
        score(3, 0)
        unit(3, "q", 3 * P, P, 1)
        ends = [score_tile(last, P), score_tile(last, 2 * P)]
        ends[0][0]()
        made[-1][0]()
        ends.append(score_tile(last, 3 * P, 2))
        ends[1][0]()
        ends[2][0]()
